import numpy as np
import ml_dtypes


def mxq(x, axis, fmt="e4m3"):
    dtype, down = {"e4m3": (ml_dtypes.float8_e4m3fn, 7), "e5m2": (ml_dtypes.float8_e5m2, 14)}[fmt]
    v = np.moveaxis(np.asarray(x, np.float32).astype(ml_dtypes.bfloat16).astype(np.float64), axis, -1)
    blocks = v.reshape(v.shape[:-1] + (-1, 32))
    amax = np.abs(blocks).max(-1, keepdims=True)
    byte = np.maximum(np.where(amax > 0, np.frexp(amax)[1] - 1 + 127, 0) - down, 1)
    scale = np.exp2(byte - 127.0)
    codes = (blocks / scale).astype(np.float32).astype(dtype).astype(np.float64)
    return np.moveaxis((codes * scale).reshape(v.shape), -1, axis)


WIDE = False


def mx_kscale(k):
    if not WIDE:
        return np.ones(k)
    levels = np.array([10, -10, 5, -5, 0])
    if k % 512:
        return np.exp2(np.random.permutation(np.resize(levels, k // 32))).repeat(32)
    a = np.empty((k // 512, 16))
    for p in range(k // 512):
        a[p, :8] = np.random.permutation(np.resize(levels, 8))
        for g in range(8):
            far = levels[np.abs(levels - a[p, g]) >= 10]
            a[p, g + 8] = far[np.random.randint(len(far))]
    return np.exp2(a.ravel()).repeat(32)


BF16 = ml_dtypes.bfloat16


def bf(x):
    return np.asarray(x, np.float32).astype(BF16)


def f64(x):
    return np.asarray(x).astype(np.float64)


E2M1 = np.array([0.0, 0.5, 1.0, 1.5, 2.0, 3.0, 4.0, 6.0, -0.0, -0.5, -1.0, -1.5, -2.0, -3.0, -4.0, -6.0])


def pack_weight(w, fmt):
    k, n = w.shape
    w = f64(bf(w)).reshape(k // 32, 32, n)
    amax = np.abs(w).max(1)
    if fmt == "e4m3":
        byte = np.frexp(amax)[1] - 1 + 127 - 7
    else:
        mant, ex = np.frexp(amax / 6.0)
        byte = np.where(mant > 0.5, ex, ex - 1) + 127
    byte = np.clip(np.where(amax > 0, byte, 1), 1, 254)
    scaled = (w * np.exp2(127.0 - byte)[:, None, :]).reshape(k, n).astype(np.float32)
    by_word = np.ascontiguousarray(scaled.reshape(k // 512, 128, 4, n).transpose(0, 1, 3, 2))
    if fmt == "e4m3":
        words = by_word.astype(ml_dtypes.float8_e4m3fn).view(np.uint8)
    else:
        c = by_word.astype(ml_dtypes.float4_e2m1fn).view(np.uint8) & 0xF
        words = c[..., 0::2] | (c[..., 1::2] << 4)
    return np.ascontiguousarray(words), np.ascontiguousarray(byte.astype(np.uint8).reshape(k // 512, 16, n))


def unpack_weight(words, scales, fmt):
    g, p, n, _ = words.shape
    if fmt == "e4m3":
        vals = np.ascontiguousarray(words).view(ml_dtypes.float8_e4m3fn).astype(np.float64)
    else:
        nib = np.empty((g, p, n, 4), np.uint8)
        nib[..., 0::2] = words & 0xF
        nib[..., 1::2] = words >> 4
        vals = E2M1[nib]
    vals = vals * np.repeat(np.exp2(scales.astype(np.float64) - 127.0), 8, axis=1)[..., None]
    return vals.transpose(0, 1, 3, 2).reshape(g * 512, n)


N, DIN, H1, H2, C, NC, G = 1024, 512, 512, 256, 128, 512, 8


def draw0():
    s, t = mx_kscale(N), mx_kscale(DIN)
    F_ = bf(np.random.uniform(size=(N, N)) * 2.0 / np.sqrt(N) * s)
    X = bf(np.random.standard_normal((N, DIN)) / s[:, None] * t)
    words, scales = pack_weight(np.random.standard_normal((DIN, H1)) * 0.8 / np.sqrt(DIN) / t[:, None], "e4m3")
    return {"F_": F_,
            "X": X,
            "W1_words": words,
            "W1_scales": scales,
            "b1": bf(np.random.standard_normal(H1) * 0.3)}


def core(F_, X, W1_words, W1_scales, b1):
    agg = mxq(f64(F_), 1, "e4m3") @ mxq(f64(X), 0, "e4m3")
    return np.tanh((mxq(agg, 1, "e4m3") @ unpack_weight(W1_words, W1_scales, "e4m3")) + f64(b1))


def e4m3fn_bytes(y):
    return np.clip(np.asarray(y, np.float64), -448.0, 448.0).astype(np.float32).astype(ml_dtypes.float8_e4m3fn).view(np.uint8)


def e4m3fn_values(b):
    return np.asarray(b, np.uint8).view(ml_dtypes.float8_e4m3fn).astype(np.float64)


def setup_inputs():
    d = draw0()
    x0 = np.asarray(d['F_']).astype(np.float64)
    s = (np.max(np.abs(x0), axis=(0,), keepdims=True) / 448.0).astype(np.float32)
    out = {}
    for k, v in d.items():
        if k == 'F_':
            out['F__bytes'] = e4m3fn_bytes(x0 / s.astype(np.float64))
            out['F__scale'] = s
        else:
            out[k] = v
    return out


def reference(F__bytes, F__scale, X, W1_words, W1_scales, b1):
    return core(e4m3fn_values(F__bytes) * F__scale.astype(np.float64), X, W1_words, W1_scales, b1)

@@ -1,0 +1,171 @@
+from contextlib import ExitStack
+
+import concourse.mybir as mybir
+from concourse.masks import make_identity
+
+F32 = mybir.dt.float32
+BF16 = mybir.dt.bfloat16
+U32 = mybir.dt.uint32
+I32 = mybir.dt.int32
+U8 = mybir.dt.uint8
+FP8 = mybir.dt.float8_e4m3fn
+FP8X4 = mybir.dt.float8_e4m3fn_x4
+MULT = mybir.AluOpType.mult
+ADD = mybir.AluOpType.add
+ACT = mybir.ActivationFunctionType
+
+P = 128
+NODES = 1024
+DIN = 512
+H = 512
+G = 2
+T = 4
+TILES = 8
+FLOPS = 2 * NODES * NODES * DIN + 2 * NODES * DIN * H
+
+
+def tile_controencodnet_pa_w8_kernel(tc, f_bytes, f_scale, x, w_words, w_scales, b1, out):
+    nc = tc.nc
+    with ExitStack() as ctx:
+        keep = ctx.enter_context(tc.tile_pool(name="keep", bufs=1))
+        ring = ctx.enter_context(tc.tile_pool(name="ring", bufs=6))
+        ps_t = ctx.enter_context(tc.psum_pool(name="ps_t", bufs=3))
+        ps_a = ctx.enter_context(tc.psum_pool(name="ps_a", bufs=2))
+        ps_o = ctx.enter_context(tc.psum_pool(name="ps_o", bufs=3))
+        ctx.enter_context(tc.manual_schedule())
+
+        bytes_src = f_bytes.rearrange("(p i) k -> p i k", i=TILES)
+        out_dst = out.rearrange("(p i) h -> p i h", i=TILES)
+        x_src = x.rearrange("(g p j) d -> g p j d", g=G, j=T)
+
+        loads = [(0, 1), (1, 2), (2, 4), (4, 6), (6, 8)]
+        fb = [keep.tile([P, (b - a) * NODES], U8, name="fb%d" % a, align_bytes=64) for a, b in loads]
+        where = {}
+        for q, (a, b) in enumerate(loads):
+            for i in range(a, b):
+                where[i] = (q, i - a)
+        fs = keep.tile([P, G, T], F32)
+        xr = [keep.tile([P, T, DIN], BF16, name="xr%d" % g, align_bytes=64) for g in range(G)]
+        xg = [keep.tile([P, T * P * T], BF16, name="xg%d" % g, align_bytes=64) for g in range(G)]
+        xc = [keep.tile([P, DIN], U32, name="xc%d" % g, align_bytes=64) for g in range(G)]
+        xs = [keep.tile([P, DIN], U8, name="xs%d" % g, align_bytes=64) for g in range(G)]
+        wc = keep.tile([P, H * T], U8, align_bytes=64)
+        ws = keep.tile([P, H], U8, align_bytes=64)
+        bias = keep.tile([P, H], BF16)
+        ident = keep.tile([P, P], F32)
+        warm = keep.tile([P, 1], F32)
+
+        def load_f(q):
+            a, b = loads[q]
+            nc.sync.dma_start(out=fb[q][:].rearrange("p (i k) -> p i k", i=b - a), in_=bytes_src[:, a:b, :])
+
+        load_f(0)
+        nc.sync.dma_start(out=fs[:], in_=f_scale.rearrange("o (g p t) -> p (o g) t", g=G, t=T))
+        nc.sync.dma_start(out=xr[0][:], in_=x_src[0])
+        load_f(1)
+        nc.sync.dma_start(out=xr[1][:], in_=x_src[1])
+        load_f(2)
+        nc.vector.memset(warm[:], 0.0)
+        nc.scalar.activation(out=warm[:], in_=warm[:], func=ACT.Tanh)
+        make_identity(nc, ident[:])
+        nc.gpsimd.memset(ws[:].bitcast(U32), 0)
+        load_f(3)
+        nc.sync.dma_start(out=wc[:], in_=w_words[0].rearrange("p n t -> p (n t)"))
+        for q in range(4):
+            nc.sync.dma_start(out=ws[32 * q : 32 * q + 4, :].bitcast(I32), in_=w_scales[0, 4 * q : 4 * q + 4, :].bitcast(I32))
+        load_f(4)
+        nc.sync.dma_start(out=bias[:], in_=b1.partition_broadcast(P))
+
+        wide, turned, fg, fc, fsc = {}, {}, {}, {}, {}
+        agg, ag, ac, asc, prod, summed, res = {}, {}, {}, {}, {}, {}, {}
+
+        def cast(i):
+            q, k = where[i]
+            wide[i] = ring.tile([P, NODES], BF16, name="wide", align_bytes=64)
+            nc.scalar.copy(out=wide[i][:], in_=fb[q][:, k * NODES : (k + 1) * NODES].bitcast(FP8))
+
+        def turn(i):
+            turned[i] = ps_t.tile([P, 2, G, P], F32, name="turned")
+            words = wide[i][:].bitcast(F32)
+            for g in range(G):
+                for u in range(2):
+                    nc.tensor.transpose(turned[i][:, u, g, :], words[:, 256 * g + u : 256 * (g + 1) : 2], ident[:])
+
+        def multiply(i):
+            fg[i] = ring.tile([P, G, P * T], BF16, name="fg", align_bytes=64)
+            nc.vector.tensor_tensor(
+                out=fg[i][:].rearrange("p g (n u e) -> p g n u e", u=2, e=2),
+                in0=turned[i][:].rearrange("p u g n -> p (u g n)").bitcast(BF16).rearrange("p (u g n e) -> p g n u e", u=2, g=G, e=2),
+                in1=fs[:].unsqueeze(2).to_broadcast([P, G, P, T]).rearrange("p g n (u e) -> p g n u e", u=2),
+                op=MULT,
+            )
+
+        def quantize_f(i):
+            fc[i] = ring.tile([P, G * P], U32, name="fc", align_bytes=64)
+            fsc[i] = ring.tile([P, G * P], U8, name="fsc", align_bytes=64)
+            nc.vector.quantize_mx(out=fc[i][:].bitcast(FP8X4), scales=fsc[i][:], in_=fg[i][:].rearrange("p g n -> p (g n)"))
+
+        def interleave_x(g, t0, t1, engine):
+            dst = xg[g][:].rearrange("p (t m j) -> p t m j", t=T, j=T)[:, t0:t1]
+            src = xr[g][:].rearrange("p j (m t) -> p t m j", t=T)[:, t0:t1]
+            if engine == "v":
+                nc.vector.tensor_copy(out=dst, in_=src)
+            elif engine == "s":
+                nc.scalar.copy(out=dst, in_=src)
+            else:
+                nc.gpsimd.tensor_scalar(out=dst, in0=src, scalar1=1.0, scalar2=0.0, op0=MULT, op1=ADD)
+
+        def quantize_x(g):
+            nc.vector.quantize_mx(out=xc[g][:].bitcast(FP8X4), scales=xs[g][:], in_=xg[g][:])
+
+        def mm1(i):
+            agg[i] = ps_a.tile([P, T, P], F32, name="agg")
+            for t in range(T):
+                cols = slice(P * t, P * (t + 1))
+                for g in range(G):
+                    rows = slice(P * g, P * (g + 1))
+                    nc.tensor.matmul_mx(out=agg[i][:, t, :], lhsT=xc[g][:, cols].bitcast(FP8X4), lhsT_scale=xs[g][:, cols],
+                                        rhs=fc[i][:, rows].bitcast(FP8X4), rhs_scale=fsc[i][:, rows], start=(g == 0), stop=(g == G - 1))
+
+        def evacuate(i):
+            ag[i] = ring.tile([P, P * T], BF16, name="ag", align_bytes=64)
+            nc.scalar.copy(out=ag[i][:].rearrange("p (n t) -> p n t", t=T), in_=agg[i][:].rearrange("p t n -> p n t"))
+
+        def quantize_a(i):
+            ac[i] = ring.tile([P, P], U32, name="ac", align_bytes=64)
+            asc[i] = ring.tile([P, P], U8, name="asc", align_bytes=64)
+            nc.vector.quantize_mx(out=ac[i][:].bitcast(FP8X4), scales=asc[i][:], in_=ag[i][:])
+
+        def mm2(i):
+            prod[i] = ps_o.tile([P, H], F32, name="prod")
+            nc.tensor.matmul_mx(out=prod[i][:], lhsT=ac[i][:].bitcast(FP8X4), lhsT_scale=asc[i][:], rhs=wc[:].bitcast(FP8X4), rhs_scale=ws[:], start=True, stop=True)
+
+        def column_parts(i):
+            return [(0, H // 2), (H // 2, H)] if i == TILES - 1 else [(0, H)]
+
+        def add_bias(i):
+            summed[i] = ring.tile([P, H], F32, name="summed")
+            for a, b in column_parts(i):
+                nc.vector.tensor_tensor(out=summed[i][:, a:b], in0=prod[i][:, a:b], in1=bias[:, a:b], op=ADD)
+
+        def finish(i):
+            res[i] = ring.tile([P, H], F32, name="res")
+            for a, b in column_parts(i):
+                nc.scalar.activation(out=res[i][:, a:b], in_=summed[i][:, a:b], func=ACT.Tanh)
+                nc.sync.dma_start(out=out_dst[:, i, a:b], in_=res[i][:, a:b])
+
+        steps = [(turn, -1), (evacuate, 5), (quantize_f, 2), (cast, -2), (multiply, 0), (mm2, 7), (quantize_a, 5), (finish, 9), (add_bias, 7), (mm1, 3)]
+        for s in range(-2, TILES + 9):
+            if s == -2:
+                interleave_x(0, 0, 4, "v")
+            if s == 0:
+                interleave_x(1, 0, 2, "s")
+            if s == 1:
+                quantize_x(0)
+            if s == 2:
+                interleave_x(1, 2, 4, "s")
+            if s == 3:
+                quantize_x(1)
+            for call, lag in steps:
+                if 0 <= s - lag < TILES:
+                    call(s - lag)

@@ -28,10 +28,8 @@ def tile_controencodnet_pa_w8_kernel(tc, f_bytes, f_scale, x, w_words, w_scales,
     nc = tc.nc
     with ExitStack() as ctx:
         keep = ctx.enter_context(tc.tile_pool(name="keep", bufs=1))
-        ring = ctx.enter_context(tc.tile_pool(name="ring", bufs=6))
-        ps_t = ctx.enter_context(tc.psum_pool(name="ps_t", bufs=3))
-        ps_a = ctx.enter_context(tc.psum_pool(name="ps_a", bufs=2))
-        ps_o = ctx.enter_context(tc.psum_pool(name="ps_o", bufs=3))
+        ring = ctx.enter_context(tc.tile_pool(name="ring", bufs=TILES))
+        ps = ctx.enter_context(tc.psum_pool(name="ps", bufs=1))
         ctx.enter_context(tc.manual_schedule())
 
         bytes_src = f_bytes.rearrange("(p i) k -> p i k", i=TILES)
@@ -44,82 +42,109 @@ def tile_controencodnet_pa_w8_kernel(tc, f_bytes, f_scale, x, w_words, w_scales,
         for q, (a, b) in enumerate(loads):
             for i in range(a, b):
                 where[i] = (q, i - a)
-        fs = keep.tile([P, G, T], F32)
+        fs = keep.tile([P, G, 2 * T], F32, name="fs")
         xr = [keep.tile([P, T, DIN], BF16, name="xr%d" % g, align_bytes=64) for g in range(G)]
         xg = [keep.tile([P, T * P * T], BF16, name="xg%d" % g, align_bytes=64) for g in range(G)]
         xc = [keep.tile([P, DIN], U32, name="xc%d" % g, align_bytes=64) for g in range(G)]
         xs = [keep.tile([P, DIN], U8, name="xs%d" % g, align_bytes=64) for g in range(G)]
-        wc = keep.tile([P, H * T], U8, align_bytes=64)
-        ws = keep.tile([P, H], U8, align_bytes=64)
-        bias = keep.tile([P, H], BF16)
-        ident = keep.tile([P, P], F32)
-        warm = keep.tile([P, 1], F32)
+        wc = keep.tile([P, H * T], U8, name="wc", align_bytes=64)
+        ws = keep.tile([P, H], U8, name="ws", align_bytes=64)
+        bias = keep.tile([P, H], BF16, name="bias")
+        ident = keep.tile([P, P], F32, name="ident")
+        ident_bf = keep.tile([P, P], BF16, name="ident_bf")
+        warm = keep.tile([P, 1], F32, name="warm")
 
         def load_f(q):
             a, b = loads[q]
             nc.sync.dma_start(out=fb[q][:].rearrange("p (i k) -> p i k", i=b - a), in_=bytes_src[:, a:b, :])
 
+        def load_scale():
+            nc.sync.dma_start(out=fs[:, :, 0:T], in_=f_scale.rearrange("o (g p t) -> p (o g) t", g=G, t=T))
+
+        def load_x(g):
+            nc.sync.dma_start(out=xr[g][:], in_=x_src[g])
+
+        def load_w():
+            nc.sync.dma_start(out=wc[:], in_=w_words[0].rearrange("p n t -> p (n t)"))
+
+        def load_w_scales():
+            for q in range(4):
+                nc.sync.dma_start(out=ws[32 * q : 32 * q + 4, :].bitcast(I32), in_=w_scales[0, 4 * q : 4 * q + 4, :].bitcast(I32))
+
+        def load_bias():
+            nc.sync.dma_start(out=bias[:], in_=b1.partition_broadcast(P))
+
+        make_identity(nc, ident[:])
+        nc.vector.memset(ws[:].bitcast(I32), 0)
         load_f(0)
-        nc.sync.dma_start(out=fs[:], in_=f_scale.rearrange("o (g p t) -> p (o g) t", g=G, t=T))
-        nc.sync.dma_start(out=xr[0][:], in_=x_src[0])
+        load_scale()
         load_f(1)
-        nc.sync.dma_start(out=xr[1][:], in_=x_src[1])
         load_f(2)
+        load_x(0)
+        load_x(1)
+        load_f(3)
+        load_w()
+        load_f(4)
+        load_w_scales()
+        load_bias()
         nc.vector.memset(warm[:], 0.0)
         nc.scalar.activation(out=warm[:], in_=warm[:], func=ACT.Tanh)
-        make_identity(nc, ident[:])
-        nc.gpsimd.memset(ws[:].bitcast(U32), 0)
-        load_f(3)
-        nc.sync.dma_start(out=wc[:], in_=w_words[0].rearrange("p n t -> p (n t)"))
-        for q in range(4):
-            nc.sync.dma_start(out=ws[32 * q : 32 * q + 4, :].bitcast(I32), in_=w_scales[0, 4 * q : 4 * q + 4, :].bitcast(I32))
-        load_f(4)
-        nc.sync.dma_start(out=bias[:], in_=b1.partition_broadcast(P))
+        nc.vector.tensor_copy(out=ident_bf[:], in_=ident[:])
 
-        wide, turned, fg, fc, fsc = {}, {}, {}, {}, {}
+        xp, wide, turned, fg, fc, fsc = {}, {}, {}, {}, {}, {}
         agg, ag, ac, asc, prod, summed, res = {}, {}, {}, {}, {}, {}, {}
 
-        def cast(i):
+        def cast(i, g0=0, g1=G):
             q, k = where[i]
-            wide[i] = ring.tile([P, NODES], BF16, name="wide", align_bytes=64)
-            nc.scalar.copy(out=wide[i][:], in_=fb[q][:, k * NODES : (k + 1) * NODES].bitcast(FP8))
+            if g0 == 0:
+                wide[i] = ring.tile([P, NODES], BF16, name="wide", align_bytes=64)
+            nc.scalar.copy(out=wide[i][:, DIN * g0 : DIN * g1], in_=fb[q][:, k * NODES + DIN * g0 : k * NODES + DIN * g1].bitcast(FP8))
 
-        def turn(i):
-            turned[i] = ps_t.tile([P, 2, G, P], F32, name="turned")
+        def turn(i, g0=0, g1=G):
+            turned[i, g0] = ps.tile([P, 2, g1 - g0, P], F32, name="turned", bufs=3)
             words = wide[i][:].bitcast(F32)
-            for g in range(G):
+            for g in range(g0, g1):
                 for u in range(2):
-                    nc.tensor.transpose(turned[i][:, u, g, :], words[:, 256 * g + u : 256 * (g + 1) : 2], ident[:])
+                    nc.tensor.transpose(turned[i, g0][:, u, g - g0, :], words[:, 256 * g + u : 256 * (g + 1) : 2], ident[:])
 
-        def multiply(i):
-            fg[i] = ring.tile([P, G, P * T], BF16, name="fg", align_bytes=64)
+        def multiply(i, g0=0, g1=G):
+            if g0 == 0:
+                fg[i] = ring.tile([P, G * P * T], BF16, name="fg", align_bytes=64)
+            n = g1 - g0
             nc.vector.tensor_tensor(
-                out=fg[i][:].rearrange("p g (n u e) -> p g n u e", u=2, e=2),
-                in0=turned[i][:].rearrange("p u g n -> p (u g n)").bitcast(BF16).rearrange("p (u g n e) -> p g n u e", u=2, g=G, e=2),
-                in1=fs[:].unsqueeze(2).to_broadcast([P, G, P, T]).rearrange("p g n (u e) -> p g n u e", u=2),
+                out=fg[i][:, DIN * g0 : DIN * g1].rearrange("p (g n u e) -> p g n u e", g=n, u=2, e=2),
+                in0=turned[i, g0][:].rearrange("p u g n -> p (u g n)").bitcast(BF16).rearrange("p (u g n e) -> p g n u e", u=2, g=n, e=2),
+                in1=fs[:, g0:g1, 0:T].unsqueeze(2).to_broadcast([P, n, P, T]).rearrange("p g n (u e) -> p g n u e", u=2),
                 op=MULT,
             )
 
         def quantize_f(i):
             fc[i] = ring.tile([P, G * P], U32, name="fc", align_bytes=64)
             fsc[i] = ring.tile([P, G * P], U8, name="fsc", align_bytes=64)
-            nc.vector.quantize_mx(out=fc[i][:].bitcast(FP8X4), scales=fsc[i][:], in_=fg[i][:].rearrange("p g n -> p (g n)"))
+            nc.vector.quantize_mx(out=fc[i][:].bitcast(FP8X4), scales=fsc[i][:], in_=fg[i][:])
 
         def interleave_x(g, t0, t1, engine):
             dst = xg[g][:].rearrange("p (t m j) -> p t m j", t=T, j=T)[:, t0:t1]
             src = xr[g][:].rearrange("p j (m t) -> p t m j", t=T)[:, t0:t1]
             if engine == "v":
                 nc.vector.tensor_copy(out=dst, in_=src)
-            elif engine == "s":
-                nc.scalar.copy(out=dst, in_=src)
             else:
-                nc.gpsimd.tensor_scalar(out=dst, in0=src, scalar1=1.0, scalar2=0.0, op0=MULT, op1=ADD)
+                nc.scalar.copy(out=dst, in_=src)
+
+        def x_matmul(g, h):
+            xp[g, h] = ps.tile([P, 2, P * T], BF16, name="prod", bufs=3)
+            src = xr[g][:].rearrange("p j (m t) -> p t m j", t=T)
+            for u in range(2):
+                nc.tensor.matmul(out=xp[g, h][:, u, :], lhsT=ident_bf[:], rhs=src[:, 2 * h + u], start=True, stop=True)
+
+        def x_copy(g, h):
+            nc.scalar.copy(out=xg[g][:, 1024 * h : 1024 * (h + 1)], in_=xp[g, h][:].rearrange("p u n -> p (u n)"))
 
         def quantize_x(g):
             nc.vector.quantize_mx(out=xc[g][:].bitcast(FP8X4), scales=xs[g][:], in_=xg[g][:])
 
         def mm1(i):
-            agg[i] = ps_a.tile([P, T, P], F32, name="agg")
+            agg[i] = ps.tile([P, T, P], F32, name="agg", bufs=2)
             for t in range(T):
                 cols = slice(P * t, P * (t + 1))
                 for g in range(G):
@@ -137,7 +162,7 @@ def tile_controencodnet_pa_w8_kernel(tc, f_bytes, f_scale, x, w_words, w_scales,
             nc.vector.quantize_mx(out=ac[i][:].bitcast(FP8X4), scales=asc[i][:], in_=ag[i][:])
 
         def mm2(i):
-            prod[i] = ps_o.tile([P, H], F32, name="prod")
+            prod[i] = ps.tile([P, H], F32, name="prod", bufs=3)
             nc.tensor.matmul_mx(out=prod[i][:], lhsT=ac[i][:].bitcast(FP8X4), lhsT_scale=asc[i][:], rhs=wc[:].bitcast(FP8X4), rhs_scale=ws[:], start=True, stop=True)
 
         def column_parts(i):
@@ -154,18 +179,94 @@ def tile_controencodnet_pa_w8_kernel(tc, f_bytes, f_scale, x, w_words, w_scales,
                 nc.scalar.activation(out=res[i][:, a:b], in_=summed[i][:, a:b], func=ACT.Tanh)
                 nc.sync.dma_start(out=out_dst[:, i, a:b], in_=res[i][:, a:b])
 
-        steps = [(turn, -1), (evacuate, 5), (quantize_f, 2), (cast, -2), (multiply, 0), (mm2, 7), (quantize_a, 5), (finish, 9), (add_bias, 7), (mm1, 3)]
-        for s in range(-2, TILES + 9):
-            if s == -2:
-                interleave_x(0, 0, 4, "v")
-            if s == 0:
-                interleave_x(1, 0, 2, "s")
-            if s == 1:
-                quantize_x(0)
-            if s == 2:
-                interleave_x(1, 2, 4, "s")
-            if s == 3:
-                quantize_x(1)
-            for call, lag in steps:
-                if 0 <= s - lag < TILES:
-                    call(s - lag)
+        cast(0, 0, 1)
+        turn(0, 0, 1)
+        multiply(0, 0, 1)
+        cast(0, 1, 2)
+        turn(0, 1, 2)
+        multiply(0, 1, 2)
+        cast(1)
+        turn(1)
+        multiply(1)
+        cast(2)
+        turn(2)
+        quantize_f(0)
+        cast(3)
+        x_matmul(0, 1)
+        multiply(2)
+        interleave_x(0, 0, 2, "s")
+        turn(3)
+        quantize_f(1)
+        interleave_x(1, 0, 2, "s")
+        x_matmul(1, 1)
+        multiply(3)
+        cast(4)
+        turn(4)
+        x_copy(0, 1)
+        quantize_x(0)
+        x_copy(1, 1)
+        quantize_x(1)
+        cast(5)
+        turn(5)
+        quantize_f(2)
+        cast(6)
+        mm1(0)
+        multiply(4)
+        cast(7)
+        turn(6)
+        quantize_f(3)
+        evacuate(0)
+        mm1(1)
+        multiply(5)
+        evacuate(1)
+        mm1(2)
+        quantize_f(4)
+        evacuate(2)
+        quantize_a(0)
+        mm2(0)
+        multiply(6)
+        turn(7)
+        quantize_f(5)
+        mm1(3)
+        quantize_a(1)
+        mm2(1)
+        add_bias(0)
+        finish(0)
+        mm1(4)
+        quantize_a(2)
+        evacuate(3)
+        mm2(2)
+        multiply(7)
+        evacuate(4)
+        mm1(5)
+        quantize_f(6)
+        evacuate(5)
+        mm1(6)
+        add_bias(1)
+        finish(1)
+        quantize_a(3)
+        evacuate(6)
+        mm2(3)
+        quantize_f(7)
+        mm1(7)
+        quantize_a(4)
+        evacuate(7)
+        mm2(4)
+        add_bias(2)
+        finish(2)
+        quantize_a(5)
+        mm2(5)
+        add_bias(3)
+        finish(3)
+        quantize_a(6)
+        mm2(6)
+        add_bias(4)
+        finish(4)
+        quantize_a(7)
+        mm2(7)
+        add_bias(5)
+        finish(5)
+        add_bias(6)
+        finish(6)
+        add_bias(7)
+        finish(7)

@@ -94,11 +94,15 @@ def tile_controencodnet_pa_w8_kernel(tc, f_bytes, f_scale, x, w_words, w_scales,
         xp, wide, turned, fg, fc, fsc = {}, {}, {}, {}, {}, {}
         agg, ag, ac, asc, prod, summed, res = {}, {}, {}, {}, {}, {}, {}
 
-        def cast(i, g0=0, g1=G):
+        def cast(i, g0=0, g1=G, on_vector=False):
             q, k = where[i]
             if g0 == 0:
                 wide[i] = ring.tile([P, NODES], BF16, name="wide", align_bytes=64)
-            nc.scalar.copy(out=wide[i][:, DIN * g0 : DIN * g1], in_=fb[q][:, k * NODES + DIN * g0 : k * NODES + DIN * g1].bitcast(FP8))
+            codes = fb[q][:, k * NODES + DIN * g0 : k * NODES + DIN * g1].bitcast(FP8)
+            if on_vector:
+                nc.vector.tensor_copy(out=wide[i][:, DIN * g0 : DIN * g1], in_=codes)
+            else:
+                nc.scalar.copy(out=wide[i][:, DIN * g0 : DIN * g1], in_=codes)
 
         def turn(i, g0=0, g1=G):
             turned[i, g0] = ps.tile([P, 2, g1 - g0, P], F32, name="turned", bufs=3)
@@ -123,34 +127,39 @@ def tile_controencodnet_pa_w8_kernel(tc, f_bytes, f_scale, x, w_words, w_scales,
             fsc[i] = ring.tile([P, G * P], U8, name="fsc", align_bytes=64)
             nc.vector.quantize_mx(out=fc[i][:].bitcast(FP8X4), scales=fsc[i][:], in_=fg[i][:])
 
-        def interleave_x(g, t0, t1, engine):
-            dst = xg[g][:].rearrange("p (t m j) -> p t m j", t=T, j=T)[:, t0:t1]
-            src = xr[g][:].rearrange("p j (m t) -> p t m j", t=T)[:, t0:t1]
+        def interleave_x(g, h, engine):
+            dst = xg[g][:].rearrange("p (t m e j) -> p m t e j", t=T, e=2, j=T)[:, 32 * h : 32 * (h + 1)]
+            src = xr[g][:].rearrange("p j (m e t) -> p m t e j", e=2, t=T)[:, 32 * h : 32 * (h + 1)]
             if engine == "v":
                 nc.vector.tensor_copy(out=dst, in_=src)
+            elif engine == "g":
+                dst = xg[g][:].rearrange("p (t m j) -> p m t j", t=T, j=T)[:, 64 * h : 64 * (h + 1)]
+                src = xr[g][:].rearrange("p j (m t) -> p m t j", t=T)[:, 64 * h : 64 * (h + 1)]
+                nc.gpsimd.tensor_scalar(out=dst, in0=src, scalar1=1.0, scalar2=0.0, op0=MULT, op1=ADD)
             else:
                 nc.scalar.copy(out=dst, in_=src)
 
         def x_matmul(g, h):
-            xp[g, h] = ps.tile([P, 2, P * T], BF16, name="prod", bufs=3)
-            src = xr[g][:].rearrange("p j (m t) -> p t m j", t=T)
+            xp[g, h] = ps.tile([P, T, 64 * T], BF16, name="prod", bufs=3)
+            src = xr[g][:].rearrange("p j (m t) -> p t m j", t=T)[:, :, 64 * h : 64 * (h + 1)]
             for u in range(2):
-                nc.tensor.matmul(out=xp[g, h][:, u, :], lhsT=ident_bf[:], rhs=src[:, 2 * h + u], start=True, stop=True)
+                nc.tensor.matmul(out=xp[g, h][:, 2 * u : 2 * u + 2, :].rearrange("p t n -> p (t n)"), lhsT=ident_bf[:], rhs=src[:, 2 * u : 2 * u + 2], start=True, stop=True)
 
         def x_copy(g, h):
-            nc.scalar.copy(out=xg[g][:, 1024 * h : 1024 * (h + 1)], in_=xp[g, h][:].rearrange("p u n -> p (u n)"))
+            nc.scalar.copy(out=xg[g][:].rearrange("p (t n) -> p t n", t=T)[:, :, 256 * h : 256 * (h + 1)], in_=xp[g, h][:])
 
         def quantize_x(g):
             nc.vector.quantize_mx(out=xc[g][:].bitcast(FP8X4), scales=xs[g][:], in_=xg[g][:])
 
-        def mm1(i):
-            agg[i] = ps.tile([P, T, P], F32, name="agg", bufs=2)
-            for t in range(T):
-                cols = slice(P * t, P * (t + 1))
-                for g in range(G):
-                    rows = slice(P * g, P * (g + 1))
+        def mm1(i, g0=0, g1=G):
+            if g0 == 0:
+                agg[i] = ps.tile([P, T, P], F32, name="agg", bufs=2)
+            for g in range(g0, g1):
+                rows = slice(P * g, P * (g + 1))
+                for t in range(T):
+                    cols = slice(P * t, P * (t + 1))
                     nc.tensor.matmul_mx(out=agg[i][:, t, :], lhsT=xc[g][:, cols].bitcast(FP8X4), lhsT_scale=xs[g][:, cols],
-                                        rhs=fc[i][:, rows].bitcast(FP8X4), rhs_scale=fsc[i][:, rows], start=(g == 0), stop=(g == G - 1))
+                                        rhs=fc[i][:, rows].bitcast(FP8X4), rhs_scale=fsc[i][:, rows], start=(g == 0 and t == 0), stop=(g == G - 1 and t == T - 1))
 
         def evacuate(i):
             ag[i] = ring.tile([P, P * T], BF16, name="ag", align_bytes=64)
@@ -179,93 +188,94 @@ def tile_controencodnet_pa_w8_kernel(tc, f_bytes, f_scale, x, w_words, w_scales,
                 nc.scalar.activation(out=res[i][:, a:b], in_=summed[i][:, a:b], func=ACT.Tanh)
                 nc.sync.dma_start(out=out_dst[:, i, a:b], in_=res[i][:, a:b])
 
+        interleave_x(0, 0, "g")
         cast(0, 0, 1)
         turn(0, 0, 1)
-        multiply(0, 0, 1)
-        cast(0, 1, 2)
-        turn(0, 1, 2)
-        multiply(0, 1, 2)
-        cast(1)
-        turn(1)
-        multiply(1)
+        cast(0, 1, 2, on_vector=True)
         cast(2)
-        turn(2)
-        quantize_f(0)
+        turn(0, 1, 2)
+        cast(1, on_vector=True)
         cast(3)
-        x_matmul(0, 1)
-        multiply(2)
-        interleave_x(0, 0, 2, "s")
+        turn(1)
+        multiply(0, 0, 1)
+        interleave_x(0, 1, "s")
+        turn(2)
+        multiply(0, 1, 2)
+        interleave_x(1, 0, "s")
         turn(3)
-        quantize_f(1)
-        interleave_x(1, 0, 2, "s")
+        multiply(1)
         x_matmul(1, 1)
-        multiply(3)
-        cast(4)
-        turn(4)
-        x_copy(0, 1)
-        quantize_x(0)
+        multiply(2)
         x_copy(1, 1)
-        quantize_x(1)
+        quantize_x(0)
+        cast(4)
+        quantize_f(0)
         cast(5)
-        turn(5)
-        quantize_f(2)
+        mm1(0, 0, 1)
+        quantize_f(1)
         cast(6)
-        mm1(0)
+        mm1(1, 0, 1)
+        multiply(3)
+        turn(4)
+        quantize_x(1)
+        mm1(0, 1, 2)
+        quantize_f(2)
+        evacuate(0)
+        mm1(1, 1, 2)
+        quantize_f(3)
+        evacuate(1)
+        turn(5)
         multiply(4)
         cast(7)
-        turn(6)
-        quantize_f(3)
-        evacuate(0)
-        mm1(1)
-        multiply(5)
-        evacuate(1)
         mm1(2)
-        quantize_f(4)
-        evacuate(2)
         quantize_a(0)
+        evacuate(2)
         mm2(0)
-        multiply(6)
-        turn(7)
-        quantize_f(5)
+        quantize_f(4)
         mm1(3)
         quantize_a(1)
+        evacuate(3)
+        turn(6)
+        multiply(5)
         mm2(1)
         add_bias(0)
         finish(0)
         mm1(4)
-        quantize_a(2)
-        evacuate(3)
-        mm2(2)
-        multiply(7)
+        quantize_f(5)
         evacuate(4)
+        turn(7)
+        quantize_a(2)
+        mm2(2)
+        multiply(6)
         mm1(5)
-        quantize_f(6)
-        evacuate(5)
-        mm1(6)
         add_bias(1)
         finish(1)
+        quantize_f(6)
+        evacuate(5)
         quantize_a(3)
-        evacuate(6)
         mm2(3)
+        multiply(7)
+        mm1(6)
+        add_bias(2)
+        evacuate(6)
         quantize_f(7)
+        finish(2)
         mm1(7)
         quantize_a(4)
-        evacuate(7)
         mm2(4)
-        add_bias(2)
-        finish(2)
-        quantize_a(5)
-        mm2(5)
         add_bias(3)
         finish(3)
+        quantize_a(5)
+        evacuate(7)
+        mm2(5)
         quantize_a(6)
         mm2(6)
         add_bias(4)
         finish(4)
-        quantize_a(7)
-        mm2(7)
         add_bias(5)
         finish(5)
+        quantize_a(7)
+        mm2(7)
         add_bias(6)
         finish(6)
         add_bias(7)

@@ -50,9 +50,9 @@ def tile_controencodnet_pa_w8_kernel(tc, f_bytes, f_scale, x, w_words, w_scales,
         wc = keep.tile([P, H * T], U8, name="wc", align_bytes=64)
         ws = keep.tile([P, H], U8, name="ws", align_bytes=64)
         bias = keep.tile([P, H], BF16, name="bias")
+        bias_col = keep.tile([P, T], F32, name="bias_col")
         ident = keep.tile([P, P], F32, name="ident")
         ident_bf = keep.tile([P, P], BF16, name="ident_bf")
-        warm = keep.tile([P, 1], F32, name="warm")
 
         def load_f(q):
             a, b = loads[q]
@@ -87,10 +87,9 @@ def tile_controencodnet_pa_w8_kernel(tc, f_bytes, f_scale, x, w_words, w_scales,
         load_f(4)
         load_w_scales()
         load_bias()
-        nc.vector.memset(warm[:], 0.0)
-        nc.scalar.activation(out=warm[:], in_=warm[:], func=ACT.Tanh)
         nc.vector.tensor_copy(out=ident_bf[:], in_=ident[:])
 
+        res_t, bias_bank = {}, []
         xp, wide, turned, fg, fc, fsc = {}, {}, {}, {}, {}, {}
         agg, ag, ac, asc, prod, summed, res = {}, {}, {}, {}, {}, {}, {}
 
@@ -112,20 +111,22 @@ def tile_controencodnet_pa_w8_kernel(tc, f_bytes, f_scale, x, w_words, w_scales,
                     nc.tensor.transpose(turned[i, g0][:, u, g - g0, :], words[:, 256 * g + u : 256 * (g + 1) : 2], ident[:])
 
         def multiply(i, g0=0, g1=G):
-            if g0 == 0:
-                fg[i] = ring.tile([P, G * P * T], BF16, name="fg", align_bytes=64)
+            if g0 == 0 and i % 2 == 0:
+                fg[i // 2] = ring.tile([P, 2 * NODES], BF16, name="fg", align_bytes=64, bufs=4)
+                fc[i // 2] = ring.tile([P, 2 * G * P], U32, name="fc", align_bytes=64, bufs=4)
+                fsc[i // 2] = ring.tile([P, 2 * G * P], U8, name="fsc", align_bytes=64, bufs=4)
             n = g1 - g0
+            base = NODES * (i % 2)
             nc.vector.tensor_tensor(
-                out=fg[i][:, DIN * g0 : DIN * g1].rearrange("p (g n u e) -> p g n u e", g=n, u=2, e=2),
+                out=fg[i // 2][:, base + DIN * g0 : base + DIN * g1].rearrange("p (g n u e) -> p g n u e", g=n, u=2, e=2),
                 in0=turned[i, g0][:].rearrange("p u g n -> p (u g n)").bitcast(BF16).rearrange("p (u g n e) -> p g n u e", u=2, g=n, e=2),
                 in1=fs[:, g0:g1, 0:T].unsqueeze(2).to_broadcast([P, n, P, T]).rearrange("p g n (u e) -> p g n u e", u=2),
                 op=MULT,
             )
 
-        def quantize_f(i):
-            fc[i] = ring.tile([P, G * P], U32, name="fc", align_bytes=64)
-            fsc[i] = ring.tile([P, G * P], U8, name="fsc", align_bytes=64)
-            nc.vector.quantize_mx(out=fc[i][:].bitcast(FP8X4), scales=fsc[i][:], in_=fg[i][:])
+        def quantize_f(i, n=1):
+            a, b = G * P * (i % 2), G * P * (i % 2 + n)
+            nc.vector.quantize_mx(out=fc[i // 2][:, a:b].bitcast(FP8X4), scales=fsc[i // 2][:, a:b], in_=fg[i // 2][:, T * a : T * b])
 
         def interleave_x(g, h, engine):
             dst = xg[g][:].rearrange("p (t m e j) -> p m t e j", t=T, e=2, j=T)[:, 32 * h : 32 * (h + 1)]
@@ -155,24 +156,58 @@ def tile_controencodnet_pa_w8_kernel(tc, f_bytes, f_scale, x, w_words, w_scales,
             if g0 == 0:
                 agg[i] = ps.tile([P, T, P], F32, name="agg", bufs=2)
             for g in range(g0, g1):
-                rows = slice(P * g, P * (g + 1))
+                rows = slice(P * (G * (i % 2) + g), P * (G * (i % 2) + g + 1))
                 for t in range(T):
                     cols = slice(P * t, P * (t + 1))
                     nc.tensor.matmul_mx(out=agg[i][:, t, :], lhsT=xc[g][:, cols].bitcast(FP8X4), lhsT_scale=xs[g][:, cols],
-                                        rhs=fc[i][:, rows].bitcast(FP8X4), rhs_scale=fsc[i][:, rows], start=(g == 0 and t == 0), stop=(g == G - 1 and t == T - 1))
+                                        rhs=fc[i // 2][:, rows].bitcast(FP8X4), rhs_scale=fsc[i // 2][:, rows], start=(g == 0 and t == 0), stop=(g == G - 1 and t == T - 1))
 
         def evacuate(i):
-            ag[i] = ring.tile([P, P * T], BF16, name="ag", align_bytes=64)
-            nc.scalar.copy(out=ag[i][:].rearrange("p (n t) -> p n t", t=T), in_=agg[i][:].rearrange("p t n -> p n t"))
+            if i % 2 == 0:
+                ag[i // 2] = ring.tile([P, 2 * DIN], BF16, name="ag", align_bytes=64, bufs=4)
+                ac[i // 2] = ring.tile([P, 2 * P], U32, name="ac", align_bytes=64, bufs=4)
+                asc[i // 2] = ring.tile([P, 2 * P], U8, name="asc", align_bytes=64, bufs=4)
+            dst = ag[i // 2][:, DIN * (i % 2) : DIN * (i % 2 + 1)]
+            nc.scalar.copy(out=dst.rearrange("p (n t) -> p n t", t=T), in_=agg[i][:].rearrange("p t n -> p n t"))
 
-        def quantize_a(i):
-            ac[i] = ring.tile([P, P], U32, name="ac", align_bytes=64)
-            asc[i] = ring.tile([P, P], U8, name="asc", align_bytes=64)
-            nc.vector.quantize_mx(out=ac[i][:].bitcast(FP8X4), scales=asc[i][:], in_=ag[i][:])
+        def quantize_a(i, n=1):
+            a, b = P * (i % 2), P * (i % 2 + n)
+            nc.vector.quantize_mx(out=ac[i // 2][:, a:b].bitcast(FP8X4), scales=asc[i // 2][:, a:b], in_=ag[i // 2][:, T * a : T * b])
 
         def mm2(i):
             prod[i] = ps.tile([P, H], F32, name="prod", bufs=3)
-            nc.tensor.matmul_mx(out=prod[i][:], lhsT=ac[i][:].bitcast(FP8X4), lhsT_scale=asc[i][:], rhs=wc[:].bitcast(FP8X4), rhs_scale=ws[:], start=True, stop=True)
+            rows = slice(P * (i % 2), P * (i % 2 + 1))
+            nc.tensor.matmul_mx(out=prod[i][:], lhsT=ac[i // 2][:, rows].bitcast(FP8X4), lhsT_scale=asc[i // 2][:, rows], rhs=wc[:].bitcast(FP8X4), rhs_scale=ws[:], start=True, stop=True)
+
+        def turn_bias():
+            bank = ps.tile([P, T, P], BF16, name="prod", bufs=3)
+            for c in range(T):
+                nc.tensor.transpose(bank[:, c, :], bias[:, P * c : P * (c + 1)], ident_bf[:])
+            bias_bank.append(bank)
+
+        def copy_bias():
+            nc.scalar.copy(out=bias_col[:], in_=bias_bank[0][:, :, 0])
+
+        def mm2_turned(i, half):
+            prod[i, half] = ps.tile([P, 2, 2 * P], F32, name="prod", bufs=3)
+            for c in range(2 * half, 2 * half + 2):
+                nc.tensor.matmul_mx(out=prod[i, half][:, c % 2, :], lhsT=wc[:, T * P * c : T * P * (c + 1)].bitcast(FP8X4), lhsT_scale=ws[:, P * c : P * (c + 1)],
+                                    rhs=ac[i // 2][:].bitcast(FP8X4), rhs_scale=asc[i // 2][:], start=True, stop=True)
+
+        def finish_turned(i, half):
+            for c in range(2 * half, 2 * half + 2):
+                res_t[i, c] = ring.tile([P, 2 * P], F32, name="res_t", bufs=4)
+                nc.scalar.activation(out=res_t[i, c][:], in_=prod[i, half][:, c % 2, :], func=ACT.Tanh, bias=bias_col[:, c : c + 1])
+
+        def turn_back(i):
+            prod[i] = ps.tile([P, H], F32, name="prod", bufs=3)
+            for c in range(T):
+                nc.tensor.transpose(prod[i][:, P * c : P * (c + 1)], res_t[i - i % 2, c][:, P * (i % 2) : P * (i % 2 + 1)], ident[:])
+
+        def copy_out(i):
+            res[i] = ring.tile([P, H], F32, name="res")
+            nc.scalar.copy(out=res[i][:], in_=prod[i][:])
+            nc.sync.dma_start(out=out_dst[:, i, :], in_=res[i][:])
 
         def column_parts(i):
             return [(0, H // 2), (H // 2, H)] if i == TILES - 1 else [(0, H)]
@@ -201,80 +236,78 @@ def tile_controencodnet_pa_w8_kernel(tc, f_bytes, f_scale, x, w_words, w_scales,
         interleave_x(0, 1, "s")
         turn(2)
         multiply(0, 1, 2)
-        interleave_x(1, 0, "s")
+        cast(4)
         turn(3)
         multiply(1)
+        interleave_x(1, 0, "s")
         x_matmul(1, 1)
         multiply(2)
         x_copy(1, 1)
-        quantize_x(0)
-        cast(4)
-        quantize_f(0)
-        cast(5)
-        mm1(0, 0, 1)
-        quantize_f(1)
-        cast(6)
-        mm1(1, 0, 1)
-        multiply(3)
         turn(4)
+        quantize_f(0, 2)
+        cast(5)
+        quantize_x(0)
+        cast(6)
+        mm1(0, 0, 1)
+        multiply(3)
+        cast(7)
+        mm1(1, 0, 1)
         quantize_x(1)
+        turn_bias()
+        multiply(4)
+        turn(5)
+        quantize_f(2, 2)
         mm1(0, 1, 2)
-        quantize_f(2)
+        multiply(5)
         evacuate(0)
         mm1(1, 1, 2)
-        quantize_f(3)
         evacuate(1)
-        turn(5)
-        multiply(4)
-        cast(7)
-        mm1(2)
-        quantize_a(0)
-        evacuate(2)
-        mm2(0)
-        quantize_f(4)
-        mm1(3)
-        quantize_a(1)
-        evacuate(3)
         turn(6)
-        multiply(5)
-        mm2(1)
-        add_bias(0)
-        finish(0)
-        mm1(4)
-        quantize_f(5)
-        evacuate(4)
+        quantize_a(0, 2)
+        copy_bias()
         turn(7)
-        quantize_a(2)
-        mm2(2)
+        quantize_f(4, 2)
+        mm1(2)
         multiply(6)
-        mm1(5)
-        add_bias(1)
-        finish(1)
+        evacuate(2)
+        mm1(3)
+        evacuate(3)
+        mm2_turned(0, 0)
+        quantize_a(2, 2)
+        finish_turned(0, 0)
+        mm2_turned(0, 1)
         quantize_f(6)
-        evacuate(5)
-        quantize_a(3)
-        mm2(3)
+        finish_turned(0, 1)
+        mm1(4)
         multiply(7)
-        mm1(6)
+        evacuate(4)
+        mm1(5)
+        evacuate(5)
+        turn_back(0)
+        copy_out(0)
+        mm2(2)
         add_bias(2)
-        evacuate(6)
+        mm1(6)
         quantize_f(7)
+        evacuate(6)
+        turn_back(1)
+        quantize_a(4, 2)
         finish(2)
-        mm1(7)
-        quantize_a(4)
-        mm2(4)
-        add_bias(3)
-        finish(3)
-        quantize_a(5)
-        evacuate(7)
-        mm2(5)
+        mm2(3)
         quantize_a(6)
-        mm2(6)
+        copy_out(1)
+        mm1(7)
+        add_bias(3)
+        evacuate(7)
+        mm2(4)
         add_bias(4)
+        finish(3)
+        mm2(5)
+        quantize_a(7)
         finish(4)
+        mm2(6)
         add_bias(5)
         finish(5)
-        quantize_a(7)
         mm2(7)
         add_bias(6)
         finish(6)

@@ -44,13 +44,17 @@ def tile_controencodnet_pa_w8_kernel(tc, f_bytes, f_scale, x, w_words, w_scales,
                 where[i] = (q, i - a)
         fs = keep.tile([P, G, 2 * T], F32, name="fs")
         xr = [keep.tile([P, T, DIN], BF16, name="xr%d" % g, align_bytes=64) for g in range(G)]
-        xg = [keep.tile([P, T * P * T], BF16, name="xg%d" % g, align_bytes=64) for g in range(G)]
-        xc = [keep.tile([P, DIN], U32, name="xc%d" % g, align_bytes=64) for g in range(G)]
-        xs = [keep.tile([P, DIN], U8, name="xs%d" % g, align_bytes=64) for g in range(G)]
+        xg_all = keep.tile([P, G * T * DIN], BF16, name="xg", align_bytes=64)
+        xc_all = keep.tile([P, G * DIN], U32, name="xc", align_bytes=64)
+        xs_all = keep.tile([P, G * DIN], U8, name="xs", align_bytes=64)
+        xg = [xg_all[:, T * DIN * g : T * DIN * (g + 1)] for g in range(G)]
+        xc = [xc_all[:, DIN * g : DIN * (g + 1)] for g in range(G)]
+        xs = [xs_all[:, DIN * g : DIN * (g + 1)] for g in range(G)]
         wc = keep.tile([P, H * T], U8, name="wc", align_bytes=64)
         ws = keep.tile([P, H], U8, name="ws", align_bytes=64)
         bias = keep.tile([P, H], BF16, name="bias")
         bias_col = keep.tile([P, T], F32, name="bias_col")
+        bias_rows = keep.tile([P, P], BF16, name="bias_rows")
         ident = keep.tile([P, P], F32, name="ident")
         ident_bf = keep.tile([P, P], BF16, name="ident_bf")
 
@@ -74,7 +78,11 @@ def tile_controencodnet_pa_w8_kernel(tc, f_bytes, f_scale, x, w_words, w_scales,
         def load_bias():
             nc.sync.dma_start(out=bias[:], in_=b1.partition_broadcast(P))
 
+        def load_bias_rows():
+            nc.sync.dma_start(out=bias_rows[0:T, :], in_=b1.rearrange("(c p) -> c p", c=T))
+
         make_identity(nc, ident[:])
+        nc.vector.memset(bias_rows[:], 0.0)
         nc.vector.memset(ws[:].bitcast(I32), 0)
         load_f(0)
         load_scale()
@@ -83,6 +91,7 @@ def tile_controencodnet_pa_w8_kernel(tc, f_bytes, f_scale, x, w_words, w_scales,
         load_x(0)
         load_x(1)
         load_f(3)
+        load_bias_rows()
         load_w()
         load_f(4)
         load_w_scales()
@@ -93,22 +102,25 @@ def tile_controencodnet_pa_w8_kernel(tc, f_bytes, f_scale, x, w_words, w_scales,
         xp, wide, turned, fg, fc, fsc = {}, {}, {}, {}, {}, {}
         agg, ag, ac, asc, prod, summed, res = {}, {}, {}, {}, {}, {}, {}
 
-        def cast(i, g0=0, g1=G, on_vector=False):
+        def cast(i, g0=0, g1=G, on_vector=False, on_gpsimd=False):
             q, k = where[i]
-            if g0 == 0:
-                wide[i] = ring.tile([P, NODES], BF16, name="wide", align_bytes=64)
+            tile = ring.tile([P, DIN * (g1 - g0)], BF16, name="wide", align_bytes=64, bufs=10)
+            for g in range(g0, g1):
+                wide[i + g // G, g % G] = tile[:, DIN * (g - g0) : DIN * (g - g0 + 1)]
             codes = fb[q][:, k * NODES + DIN * g0 : k * NODES + DIN * g1].bitcast(FP8)
-            if on_vector:
-                nc.vector.tensor_copy(out=wide[i][:, DIN * g0 : DIN * g1], in_=codes)
+            if on_gpsimd:
+                nc.gpsimd.tensor_copy(out=tile[:], in_=codes)
+            elif on_vector:
+                nc.vector.tensor_copy(out=tile[:], in_=codes)
             else:
-                nc.scalar.copy(out=wide[i][:, DIN * g0 : DIN * g1], in_=codes)
+                nc.scalar.copy(out=tile[:], in_=codes)
 
         def turn(i, g0=0, g1=G):
             turned[i, g0] = ps.tile([P, 2, g1 - g0, P], F32, name="turned", bufs=3)
-            words = wide[i][:].bitcast(F32)
             for g in range(g0, g1):
+                words = wide[i, g].bitcast(F32)
                 for u in range(2):
-                    nc.tensor.transpose(turned[i, g0][:, u, g - g0, :], words[:, 256 * g + u : 256 * (g + 1) : 2], ident[:])
+                    nc.tensor.transpose(turned[i, g0][:, u, g - g0, :], words[:, u : 2 * P : 2], ident[:])
 
         def multiply(i, g0=0, g1=G):
             if g0 == 0 and i % 2 == 0:
@@ -129,12 +141,12 @@ def tile_controencodnet_pa_w8_kernel(tc, f_bytes, f_scale, x, w_words, w_scales,
             nc.vector.quantize_mx(out=fc[i // 2][:, a:b].bitcast(FP8X4), scales=fsc[i // 2][:, a:b], in_=fg[i // 2][:, T * a : T * b])
 
         def interleave_x(g, h, engine):
-            dst = xg[g][:].rearrange("p (t m e j) -> p m t e j", t=T, e=2, j=T)[:, 32 * h : 32 * (h + 1)]
+            dst = xg[g].rearrange("p (t m e j) -> p m t e j", t=T, e=2, j=T)[:, 32 * h : 32 * (h + 1)]
             src = xr[g][:].rearrange("p j (m e t) -> p m t e j", e=2, t=T)[:, 32 * h : 32 * (h + 1)]
             if engine == "v":
                 nc.vector.tensor_copy(out=dst, in_=src)
             elif engine == "g":
-                dst = xg[g][:].rearrange("p (t m j) -> p m t j", t=T, j=T)[:, 64 * h : 64 * (h + 1)]
+                dst = xg[g].rearrange("p (t m j) -> p m t j", t=T, j=T)[:, 64 * h : 64 * (h + 1)]
                 src = xr[g][:].rearrange("p j (m t) -> p m t j", t=T)[:, 64 * h : 64 * (h + 1)]
                 nc.gpsimd.tensor_scalar(out=dst, in0=src, scalar1=1.0, scalar2=0.0, op0=MULT, op1=ADD)
             else:
@@ -147,10 +159,10 @@ def tile_controencodnet_pa_w8_kernel(tc, f_bytes, f_scale, x, w_words, w_scales,
                 nc.tensor.matmul(out=xp[g, h][:, 2 * u : 2 * u + 2, :].rearrange("p t n -> p (t n)"), lhsT=ident_bf[:], rhs=src[:, 2 * u : 2 * u + 2], start=True, stop=True)
 
         def x_copy(g, h):
-            nc.scalar.copy(out=xg[g][:].rearrange("p (t n) -> p t n", t=T)[:, :, 256 * h : 256 * (h + 1)], in_=xp[g, h][:])
+            nc.scalar.copy(out=xg[g].rearrange("p (t n) -> p t n", t=T)[:, :, 256 * h : 256 * (h + 1)], in_=xp[g, h][:])
 
-        def quantize_x(g):
-            nc.vector.quantize_mx(out=xc[g][:].bitcast(FP8X4), scales=xs[g][:], in_=xg[g][:])
+        def quantize_x(g, n=1):
+            nc.vector.quantize_mx(out=xc_all[:, DIN * g : DIN * (g + n)].bitcast(FP8X4), scales=xs_all[:, DIN * g : DIN * (g + n)], in_=xg_all[:, T * DIN * g : T * DIN * (g + n)])
 
         def mm1(i, g0=0, g1=G):
             if g0 == 0:
@@ -180,48 +192,61 @@ def tile_controencodnet_pa_w8_kernel(tc, f_bytes, f_scale, x, w_words, w_scales,
             nc.tensor.matmul_mx(out=prod[i][:], lhsT=ac[i // 2][:, rows].bitcast(FP8X4), lhsT_scale=asc[i // 2][:, rows], rhs=wc[:].bitcast(FP8X4), rhs_scale=ws[:], start=True, stop=True)
 
         def turn_bias():
-            bank = ps.tile([P, T, P], BF16, name="prod", bufs=3)
-            for c in range(T):
-                nc.tensor.transpose(bank[:, c, :], bias[:, P * c : P * (c + 1)], ident_bf[:])
+            bank = ps.tile([P, P], BF16, name="prod", bufs=3)
+            nc.tensor.transpose(bank[:], bias_rows[:], ident_bf[:])
             bias_bank.append(bank)
 
         def copy_bias():
-            nc.scalar.copy(out=bias_col[:], in_=bias_bank[0][:, :, 0])
+            nc.scalar.copy(out=bias_col[:], in_=bias_bank[0][:, 0:T])
 
-        def mm2_turned(i, half):
-            prod[i, half] = ps.tile([P, 2, 2 * P], F32, name="prod", bufs=3)
-            for c in range(2 * half, 2 * half + 2):
-                nc.tensor.matmul_mx(out=prod[i, half][:, c % 2, :], lhsT=wc[:, T * P * c : T * P * (c + 1)].bitcast(FP8X4), lhsT_scale=ws[:, P * c : P * (c + 1)],
-                                    rhs=ac[i // 2][:].bitcast(FP8X4), rhs_scale=asc[i // 2][:], start=True, stop=True)
+        def mm2_turned(i, half, n=2):
+            per = 2 if n == 2 else 4
+            prod[i, half] = ps.tile([P, per, n * P], F32, name="prod", bufs=3)
+            rows = slice(P * (i % 2), P * (i % 2 + n))
+            for c in range(per * half, per * half + per):
+                nc.tensor.matmul_mx(out=prod[i, half][:, c % per, :], lhsT=wc[:, T * P * c : T * P * (c + 1)].bitcast(FP8X4), lhsT_scale=ws[:, P * c : P * (c + 1)],
+                                    rhs=ac[i // 2][:, rows].bitcast(FP8X4), rhs_scale=asc[i // 2][:, rows], start=True, stop=True)
 
-        def finish_turned(i, half):
-            for c in range(2 * half, 2 * half + 2):
-                res_t[i, c] = ring.tile([P, 2 * P], F32, name="res_t", bufs=4)
-                nc.scalar.activation(out=res_t[i, c][:], in_=prod[i, half][:, c % 2, :], func=ACT.Tanh, bias=bias_col[:, c : c + 1])
+        def finish_turned(i, half, n=2):
+            per = 2 if n == 2 else 4
+            for c in range(per * half, per * half + per):
+                tile = ring.tile([P, n * P], F32, name="res_t", bufs=8)
+                for j in range(n):
+                    res_t[i + j, c] = tile[:, P * j : P * (j + 1)]
+                nc.scalar.activation(out=tile[:], in_=prod[i, half][:, c % per, :], func=ACT.Tanh, bias=bias_col[:, c : c + 1])
 
         def turn_back(i):
             prod[i] = ps.tile([P, H], F32, name="prod", bufs=3)
             for c in range(T):
-                nc.tensor.transpose(prod[i][:, P * c : P * (c + 1)], res_t[i - i % 2, c][:, P * (i % 2) : P * (i % 2 + 1)], ident[:])
+                nc.tensor.transpose(prod[i][:, P * c : P * (c + 1)], res_t[i, c], ident[:])
 
-        def copy_out(i):
+        def copy_out(i, on_vector=False):
             res[i] = ring.tile([P, H], F32, name="res")
-            nc.scalar.copy(out=res[i][:], in_=prod[i][:])
+            if on_vector:
+                nc.vector.tensor_copy(out=res[i][:], in_=prod[i][:])
+            else:
+                nc.scalar.copy(out=res[i][:], in_=prod[i][:])
             nc.sync.dma_start(out=out_dst[:, i, :], in_=res[i][:])
 
         def column_parts(i):
             return [(0, H // 2), (H // 2, H)] if i == TILES - 1 else [(0, H)]
 
         def add_bias(i):
-            summed[i] = ring.tile([P, H], F32, name="summed")
+            if i % 2 == 0 or i // 2 not in summed:
+                summed[i // 2] = ring.tile([P, 2, H], F32, name="summed", bufs=4)
             for a, b in column_parts(i):
-                nc.vector.tensor_tensor(out=summed[i][:, a:b], in0=prod[i][:, a:b], in1=bias[:, a:b], op=ADD)
+                nc.vector.tensor_tensor(out=summed[i // 2][:, i % 2, a:b], in0=prod[i][:, a:b], in1=bias[:, a:b], op=ADD)
 
         def finish(i):
             res[i] = ring.tile([P, H], F32, name="res")
             for a, b in column_parts(i):
-                nc.scalar.activation(out=res[i][:, a:b], in_=summed[i][:, a:b], func=ACT.Tanh)
+                nc.scalar.activation(out=res[i][:, a:b], in_=summed[i // 2][:, i % 2, a:b], func=ACT.Tanh)
                 nc.sync.dma_start(out=out_dst[:, i, a:b], in_=res[i][:, a:b])
+
+        def finish_pair(i):
+            res[i] = ring.tile([P, 2, H], F32, name="res2", bufs=4)
+            nc.scalar.activation(out=res[i][:], in_=summed[i // 2][:], func=ACT.Tanh)
+            nc.sync.dma_start(out=out_dst[:, i : i + 2, :], in_=res[i][:])
 
         interleave_x(0, 0, "g")
         cast(0, 0, 1)
@@ -244,27 +269,27 @@ def tile_controencodnet_pa_w8_kernel(tc, f_bytes, f_scale, x, w_words, w_scales,
         multiply(2)
         x_copy(1, 1)
         turn(4)
-        quantize_f(0, 2)
-        cast(5)
         quantize_x(0)
-        cast(6)
+        cast(5)
+        turn_bias()
+        quantize_f(0, 2)
+        copy_bias()
         mm1(0, 0, 1)
         multiply(3)
-        cast(7)
+        cast(6)
         mm1(1, 0, 1)
         quantize_x(1)
-        turn_bias()
-        multiply(4)
+        cast(7)
         turn(5)
-        quantize_f(2, 2)
+        multiply(4)
         mm1(0, 1, 2)
-        multiply(5)
+        quantize_f(2, 2)
         evacuate(0)
         mm1(1, 1, 2)
+        multiply(5)
         evacuate(1)
         turn(6)
         quantize_a(0, 2)
-        copy_bias()
         turn(7)
         quantize_f(4, 2)
         mm1(2)
@@ -284,29 +309,29 @@ def tile_controencodnet_pa_w8_kernel(tc, f_bytes, f_scale, x, w_words, w_scales,
         mm1(5)
         evacuate(5)
         turn_back(0)
+        quantize_a(4, 2)
         copy_out(0)
         mm2(2)
-        add_bias(2)
-        mm1(6)
         quantize_f(7)
+        mm1(6)
+        add_bias(2)
         evacuate(6)
         turn_back(1)
-        quantize_a(4, 2)
-        finish(2)
-        mm2(3)
         quantize_a(6)
         copy_out(1)
-        mm1(7)
+        mm2(3)
         add_bias(3)
+        finish(2)
+        mm1(7)
         evacuate(7)
         mm2(4)
         add_bias(4)
         finish(3)
         mm2(5)
-        quantize_a(7)
+        add_bias(5)
         finish(4)
         mm2(6)
-        add_bias(5)
+        quantize_a(7)
         finish(5)
         mm2(7)
         add_bias(6)

@@ -21,6 +21,8 @@ H = 512
 G = 2
 T = 4
 TILES = 8
+BANKS = 8
+OPEN = 3
 FLOPS = 2 * NODES * NODES * DIN + 2 * NODES * DIN * H
 
 
@@ -44,10 +46,9 @@ def tile_controencodnet_pa_w8_kernel(tc, f_bytes, f_scale, x, w_words, w_scales,
                 where[i] = (q, i - a)
         fs = keep.tile([P, G, 2 * T], F32, name="fs")
         xr = [keep.tile([P, T, DIN], BF16, name="xr%d" % g, align_bytes=64) for g in range(G)]
-        xg_all = keep.tile([P, G * T * DIN], BF16, name="xg", align_bytes=64)
         xc_all = keep.tile([P, G * DIN], U32, name="xc", align_bytes=64)
         xs_all = keep.tile([P, G * DIN], U8, name="xs", align_bytes=64)
-        xg = [xg_all[:, T * DIN * g : T * DIN * (g + 1)] for g in range(G)]
+        xg = [keep.tile([P, T * DIN], BF16, name="xg%d" % g, align_bytes=64)[:] for g in range(G)]
         xc = [xc_all[:, DIN * g : DIN * (g + 1)] for g in range(G)]
         xs = [xs_all[:, DIN * g : DIN * (g + 1)] for g in range(G)]
         wc = keep.tile([P, H * T], U8, name="wc", align_bytes=64)
@@ -62,71 +63,52 @@ def tile_controencodnet_pa_w8_kernel(tc, f_bytes, f_scale, x, w_words, w_scales,
             a, b = loads[q]
             nc.sync.dma_start(out=fb[q][:].rearrange("p (i k) -> p i k", i=b - a), in_=bytes_src[:, a:b, :])
 
-        def load_scale():
-            nc.sync.dma_start(out=fs[:, :, 0:T], in_=f_scale.rearrange("o (g p t) -> p (o g) t", g=G, t=T))
-
-        def load_x(g):
-            nc.sync.dma_start(out=xr[g][:], in_=x_src[g])
-
-        def load_w():
-            nc.sync.dma_start(out=wc[:], in_=w_words[0].rearrange("p n t -> p (n t)"))
-
-        def load_w_scales():
-            for q in range(4):
-                nc.sync.dma_start(out=ws[32 * q : 32 * q + 4, :].bitcast(I32), in_=w_scales[0, 4 * q : 4 * q + 4, :].bitcast(I32))
-
-        def load_bias():
-            nc.sync.dma_start(out=bias[:], in_=b1.partition_broadcast(P))
-
-        def load_bias_rows():
-            nc.sync.dma_start(out=bias_rows[0:T, :], in_=b1.rearrange("(c p) -> c p", c=T))
-
         make_identity(nc, ident[:])
         nc.vector.memset(bias_rows[:], 0.0)
         nc.vector.memset(ws[:].bitcast(I32), 0)
+
         load_f(0)
-        load_scale()
-        load_f(1)
-        load_f(2)
-        load_x(0)
-        load_x(1)
-        load_f(3)
-        load_bias_rows()
-        load_w()
-        load_f(4)
-        load_w_scales()
-        load_bias()
+        nc.sync.dma_start(out=fs[:, :, 0:T], in_=f_scale.rearrange("o (g p t) -> p (o g) t", g=G, t=T))
+        for q in range(1, len(loads) - 1):
+            load_f(q)
+        for g in range(G):
+            nc.sync.dma_start(out=xr[g][:], in_=x_src[g])
+        load_f(len(loads) - 1)
+        nc.sync.dma_start(out=bias_rows[0:T, :], in_=b1.rearrange("(c p) -> c p", c=T))
+        nc.sync.dma_start(out=wc[:], in_=w_words[0].rearrange("p n t -> p (n t)"))
+        for q in range(4):
+            nc.sync.dma_start(out=ws[32 * q : 32 * q + 4, :].bitcast(I32), in_=w_scales[0, 4 * q : 4 * q + 4, :].bitcast(I32))
+        nc.sync.dma_start(out=bias[:], in_=b1.partition_broadcast(P))
         nc.vector.tensor_copy(out=ident_bf[:], in_=ident[:])
 
-        res_t, bias_bank = {}, []
-        xp, wide, turned, fg, fc, fsc = {}, {}, {}, {}, {}, {}
-        agg, ag, ac, asc, prod, summed, res = {}, {}, {}, {}, {}, {}, {}
+        wide, turned, fg, fc, fsc = {}, {}, {}, {}, {}
+        agg, ag, ac, asc, prod, summed, res_t = {}, {}, {}, {}, {}, {}, {}
+        for pair in range(TILES // 2):
+            fg[pair] = keep.tile([P, 2 * NODES], BF16, name="fg%d" % pair, align_bytes=64)
+            fc[pair] = keep.tile([P, 2 * G * P], U32, name="fc%d" % pair, align_bytes=64)
+            fsc[pair] = keep.tile([P, 2 * G * P], U8, name="fsc%d" % pair, align_bytes=64)
+            ag[pair] = keep.tile([P, 2 * DIN], BF16, name="ag%d" % pair, align_bytes=64)
+            ac[pair] = keep.tile([P, 2 * P], U32, name="ac%d" % pair, align_bytes=64)
+            asc[pair] = keep.tile([P, 2 * P], U8, name="asc%d" % pair, align_bytes=64)
+        for pair in range(1, TILES // 2):
+            summed[pair] = keep.tile([P, 2, H], F32, name="summed%d" % pair)
 
-        def cast(i, g0=0, g1=G, on_vector=False, on_gpsimd=False):
+        def widen(i, g0=0, g1=G, on_vector=False):
             q, k = where[i]
-            tile = ring.tile([P, DIN * (g1 - g0)], BF16, name="wide", align_bytes=64, bufs=10)
+            tile = ring.tile([P, DIN * (g1 - g0)], BF16, name="wide", align_bytes=64, bufs=TILES + 1)
             for g in range(g0, g1):
-                wide[i + g // G, g % G] = tile[:, DIN * (g - g0) : DIN * (g - g0 + 1)]
-            codes = fb[q][:, k * NODES + DIN * g0 : k * NODES + DIN * g1].bitcast(FP8)
-            if on_gpsimd:
-                nc.gpsimd.tensor_copy(out=tile[:], in_=codes)
-            elif on_vector:
-                nc.vector.tensor_copy(out=tile[:], in_=codes)
-            else:
-                nc.scalar.copy(out=tile[:], in_=codes)
+                wide[i, g] = tile[:, DIN * (g - g0) : DIN * (g - g0 + 1)]
+            copy = nc.vector.tensor_copy if on_vector else nc.scalar.copy
+            copy(out=tile[:], in_=fb[q][:, k * NODES + DIN * g0 : k * NODES + DIN * g1].bitcast(FP8))
 
         def turn(i, g0=0, g1=G):
-            turned[i, g0] = ps.tile([P, 2, g1 - g0, P], F32, name="turned", bufs=3)
+            turned[i, g0] = ps.tile([P, 2, g1 - g0, P], F32, name="bank", bufs=BANKS)
             for g in range(g0, g1):
                 words = wide[i, g].bitcast(F32)
                 for u in range(2):
                     nc.tensor.transpose(turned[i, g0][:, u, g - g0, :], words[:, u : 2 * P : 2], ident[:])
 
         def multiply(i, g0=0, g1=G):
-            if g0 == 0 and i % 2 == 0:
-                fg[i // 2] = ring.tile([P, 2 * NODES], BF16, name="fg", align_bytes=64, bufs=4)
-                fc[i // 2] = ring.tile([P, 2 * G * P], U32, name="fc", align_bytes=64, bufs=4)
-                fsc[i // 2] = ring.tile([P, 2 * G * P], U8, name="fsc", align_bytes=64, bufs=4)
             n = g1 - g0
             base = NODES * (i % 2)
             nc.vector.tensor_tensor(
@@ -140,33 +122,30 @@ def tile_controencodnet_pa_w8_kernel(tc, f_bytes, f_scale, x, w_words, w_scales,
             a, b = G * P * (i % 2), G * P * (i % 2 + n)
             nc.vector.quantize_mx(out=fc[i // 2][:, a:b].bitcast(FP8X4), scales=fsc[i // 2][:, a:b], in_=fg[i // 2][:, T * a : T * b])
 
-        def interleave_x(g, h, engine):
+        def interleave_x_gpsimd(g, h):
+            dst = xg[g].rearrange("p (t m j) -> p m t j", t=T, j=T)[:, 64 * h : 64 * (h + 1)]
+            src = xr[g][:].rearrange("p j (m t) -> p m t j", t=T)[:, 64 * h : 64 * (h + 1)]
+            nc.gpsimd.tensor_scalar(out=dst, in0=src, scalar1=1.0, scalar2=0.0, op0=MULT, op1=ADD)
+
+        def interleave_x_scalar(g, h):
             dst = xg[g].rearrange("p (t m e j) -> p m t e j", t=T, e=2, j=T)[:, 32 * h : 32 * (h + 1)]
             src = xr[g][:].rearrange("p j (m e t) -> p m t e j", e=2, t=T)[:, 32 * h : 32 * (h + 1)]
-            if engine == "v":
-                nc.vector.tensor_copy(out=dst, in_=src)
-            elif engine == "g":
-                dst = xg[g].rearrange("p (t m j) -> p m t j", t=T, j=T)[:, 64 * h : 64 * (h + 1)]
-                src = xr[g][:].rearrange("p j (m t) -> p m t j", t=T)[:, 64 * h : 64 * (h + 1)]
-                nc.gpsimd.tensor_scalar(out=dst, in0=src, scalar1=1.0, scalar2=0.0, op0=MULT, op1=ADD)
-            else:
-                nc.scalar.copy(out=dst, in_=src)
+            nc.scalar.copy(out=dst, in_=src)
 
-        def x_matmul(g, h):
-            xp[g, h] = ps.tile([P, T, 64 * T], BF16, name="prod", bufs=3)
-            src = xr[g][:].rearrange("p j (m t) -> p t m j", t=T)[:, :, 64 * h : 64 * (h + 1)]
+        def interleave_x_tensor(g, h):
+            bank = ps.tile([P, T, 64 * T], BF16, name="bank", bufs=BANKS)
+            src = xr[g][:].rearrange("p j (m t) -> p j m t", t=T)[:, :, 64 * h : 64 * (h + 1)]
+            dst = bank[:].rearrange("p t (m j) -> p j m t", j=T)
             for u in range(2):
-                nc.tensor.matmul(out=xp[g, h][:, 2 * u : 2 * u + 2, :].rearrange("p t n -> p (t n)"), lhsT=ident_bf[:], rhs=src[:, 2 * u : 2 * u + 2], start=True, stop=True)
+                nc.tensor.matmul(out=dst[:, 2 * u : 2 * u + 2], lhsT=ident_bf[:], rhs=src[:, 2 * u : 2 * u + 2], start=True, stop=True)
+            return bank
 
-        def x_copy(g, h):
-            nc.scalar.copy(out=xg[g].rearrange("p (t n) -> p t n", t=T)[:, :, 256 * h : 256 * (h + 1)], in_=xp[g, h][:])
+        def quantize_x(g):
+            nc.vector.quantize_mx(out=xc[g].bitcast(FP8X4), scales=xs[g], in_=xg[g])
 
-        def quantize_x(g, n=1):
-            nc.vector.quantize_mx(out=xc_all[:, DIN * g : DIN * (g + n)].bitcast(FP8X4), scales=xs_all[:, DIN * g : DIN * (g + n)], in_=xg_all[:, T * DIN * g : T * DIN * (g + n)])
-
-        def mm1(i, g0=0, g1=G):
+        def first_product(i, g0=0, g1=G):
             if g0 == 0:
-                agg[i] = ps.tile([P, T, P], F32, name="agg", bufs=2)
+                agg[i] = ps.tile([P, T, P], F32, name="bank", bufs=BANKS)
             for g in range(g0, g1):
                 rows = slice(P * (G * (i % 2) + g), P * (G * (i % 2) + g + 1))
                 for t in range(T):
@@ -174,167 +153,117 @@ def tile_controencodnet_pa_w8_kernel(tc, f_bytes, f_scale, x, w_words, w_scales,
                     nc.tensor.matmul_mx(out=agg[i][:, t, :], lhsT=xc[g][:, cols].bitcast(FP8X4), lhsT_scale=xs[g][:, cols],
                                         rhs=fc[i // 2][:, rows].bitcast(FP8X4), rhs_scale=fsc[i // 2][:, rows], start=(g == 0 and t == 0), stop=(g == G - 1 and t == T - 1))
 
-        def evacuate(i):
-            if i % 2 == 0:
-                ag[i // 2] = ring.tile([P, 2 * DIN], BF16, name="ag", align_bytes=64, bufs=4)
-                ac[i // 2] = ring.tile([P, 2 * P], U32, name="ac", align_bytes=64, bufs=4)
-                asc[i // 2] = ring.tile([P, 2 * P], U8, name="asc", align_bytes=64, bufs=4)
+        def empty_agg(i, on_vector=False):
             dst = ag[i // 2][:, DIN * (i % 2) : DIN * (i % 2 + 1)]
-            nc.scalar.copy(out=dst.rearrange("p (n t) -> p n t", t=T), in_=agg[i][:].rearrange("p t n -> p n t"))
+            copy = nc.vector.tensor_copy if on_vector else nc.scalar.copy
+            copy(out=dst.rearrange("p (n t) -> p n t", t=T), in_=agg[i][:].rearrange("p t n -> p n t"))
 
-        def quantize_a(i, n=1):
+        def quantize_agg(i, n=1):
             a, b = P * (i % 2), P * (i % 2 + n)
             nc.vector.quantize_mx(out=ac[i // 2][:, a:b].bitcast(FP8X4), scales=asc[i // 2][:, a:b], in_=ag[i // 2][:, T * a : T * b])
 
-        def mm2(i):
-            prod[i] = ps.tile([P, H], F32, name="prod", bufs=3)
+        def second_product(i):
+            prod[i] = ps.tile([P, H], F32, name="bank", bufs=BANKS)
             rows = slice(P * (i % 2), P * (i % 2 + 1))
             nc.tensor.matmul_mx(out=prod[i][:], lhsT=ac[i // 2][:, rows].bitcast(FP8X4), lhsT_scale=asc[i // 2][:, rows], rhs=wc[:].bitcast(FP8X4), rhs_scale=ws[:], start=True, stop=True)
 
-        def turn_bias():
-            bank = ps.tile([P, P], BF16, name="prod", bufs=3)
-            nc.tensor.transpose(bank[:], bias_rows[:], ident_bf[:])
-            bias_bank.append(bank)
+        def second_product_turned(half):
+            bank = ps.tile([P, 2, 2 * P], F32, name="bank", bufs=BANKS)
+            for c in range(2 * half, 2 * half + 2):
+                nc.tensor.matmul_mx(out=bank[:, c % 2, :], lhsT=wc[:, T * P * c : T * P * (c + 1)].bitcast(FP8X4), lhsT_scale=ws[:, P * c : P * (c + 1)],
+                                    rhs=ac[0][:].bitcast(FP8X4), rhs_scale=asc[0][:], start=True, stop=True)
+            for c in range(2 * half, 2 * half + 2):
+                res_t[c] = ring.tile([P, 2 * P], F32, name="res_t")
+                nc.scalar.activation(out=res_t[c][:], in_=bank[:, c % 2, :], func=ACT.Tanh, bias=bias_col[:, c : c + 1])
 
-        def copy_bias():
-            nc.scalar.copy(out=bias_col[:], in_=bias_bank[0][:, 0:T])
-
-        def mm2_turned(i, half, n=2):
-            per = 2 if n == 2 else 4
-            prod[i, half] = ps.tile([P, per, n * P], F32, name="prod", bufs=3)
-            rows = slice(P * (i % 2), P * (i % 2 + n))
-            for c in range(per * half, per * half + per):
-                nc.tensor.matmul_mx(out=prod[i, half][:, c % per, :], lhsT=wc[:, T * P * c : T * P * (c + 1)].bitcast(FP8X4), lhsT_scale=ws[:, P * c : P * (c + 1)],
-                                    rhs=ac[i // 2][:, rows].bitcast(FP8X4), rhs_scale=asc[i // 2][:, rows], start=True, stop=True)
-
-        def finish_turned(i, half, n=2):
-            per = 2 if n == 2 else 4
-            for c in range(per * half, per * half + per):
-                tile = ring.tile([P, n * P], F32, name="res_t", bufs=8)
-                for j in range(n):
-                    res_t[i + j, c] = tile[:, P * j : P * (j + 1)]
-                nc.scalar.activation(out=tile[:], in_=prod[i, half][:, c % per, :], func=ACT.Tanh, bias=bias_col[:, c : c + 1])
-
-        def turn_back(i):
-            prod[i] = ps.tile([P, H], F32, name="prod", bufs=3)
+        def turn_back_and_store(i):
+            bank = ps.tile([P, H], F32, name="bank", bufs=BANKS)
             for c in range(T):
-                nc.tensor.transpose(prod[i][:, P * c : P * (c + 1)], res_t[i, c], ident[:])
-
-        def copy_out(i, on_vector=False):
-            res[i] = ring.tile([P, H], F32, name="res")
-            if on_vector:
-                nc.vector.tensor_copy(out=res[i][:], in_=prod[i][:])
-            else:
-                nc.scalar.copy(out=res[i][:], in_=prod[i][:])
-            nc.sync.dma_start(out=out_dst[:, i, :], in_=res[i][:])
+                nc.tensor.transpose(bank[:, P * c : P * (c + 1)], res_t[c][:, P * i : P * (i + 1)], ident[:])
+            res = ring.tile([P, H], F32, name="res")
+            nc.scalar.copy(out=res[:], in_=bank[:])
+            nc.sync.dma_start(out=out_dst[:, i, :], in_=res[:])
 
         def column_parts(i):
             return [(0, H // 2), (H // 2, H)] if i == TILES - 1 else [(0, H)]
 
         def add_bias(i):
-            if i % 2 == 0 or i // 2 not in summed:
-                summed[i // 2] = ring.tile([P, 2, H], F32, name="summed", bufs=4)
             for a, b in column_parts(i):
                 nc.vector.tensor_tensor(out=summed[i // 2][:, i % 2, a:b], in0=prod[i][:, a:b], in1=bias[:, a:b], op=ADD)
 
-        def finish(i):
-            res[i] = ring.tile([P, H], F32, name="res")
+        def tanh_and_store(i):
+            res = ring.tile([P, H], F32, name="res")
             for a, b in column_parts(i):
-                nc.scalar.activation(out=res[i][:, a:b], in_=summed[i // 2][:, i % 2, a:b], func=ACT.Tanh)
-                nc.sync.dma_start(out=out_dst[:, i, a:b], in_=res[i][:, a:b])
+                nc.scalar.activation(out=res[:, a:b], in_=summed[i // 2][:, i % 2, a:b], func=ACT.Tanh)
+                nc.sync.dma_start(out=out_dst[:, i, a:b], in_=res[:, a:b])
 
-        def finish_pair(i):
-            res[i] = ring.tile([P, 2, H], F32, name="res2", bufs=4)
-            nc.scalar.activation(out=res[i][:], in_=summed[i // 2][:], func=ACT.Tanh)
-            nc.sync.dma_start(out=out_dst[:, i : i + 2, :], in_=res[i][:])
+        interleave_x_gpsimd(0, 0)
+        widen(0, 0, 1)
+        widen(0, 1, 2, on_vector=True)
+        widen(1, on_vector=True)
+        for g in range(G):
+            turn(0, g, g + 1)
+            multiply(0, g, g + 1)
+        for i in range(2, 6):
+            widen(i)
+        for i in range(1, 4):
+            turn(i)
+            multiply(i)
+        x_bank = interleave_x_tensor(1, 1)
+        for i in (4, 5):
+            turn(i)
+        bias_bank = ps.tile([P, P], BF16, name="bank", bufs=BANKS)
+        nc.tensor.transpose(bias_bank[:], bias_rows[:], ident_bf[:])
+        interleave_x_scalar(0, 1)
+        interleave_x_scalar(1, 0)
+        nc.scalar.copy(out=xg[1].rearrange("p (t n) -> p t n", t=T)[:, :, 2 * P : T * P], in_=x_bank[:])
+        nc.scalar.copy(out=bias_col[:], in_=bias_bank[:, 0:T])
+        for i in (6, 7):
+            widen(i)
 
-        interleave_x(0, 0, "g")
-        cast(0, 0, 1)
-        turn(0, 0, 1)
-        cast(0, 1, 2, on_vector=True)
-        cast(2)
-        turn(0, 1, 2)
-        cast(1, on_vector=True)
-        cast(3)
-        turn(1)
-        multiply(0, 0, 1)
-        interleave_x(0, 1, "s")
-        turn(2)
-        multiply(0, 1, 2)
-        cast(4)
-        turn(3)
-        multiply(1)
-        interleave_x(1, 0, "s")
-        x_matmul(1, 1)
-        multiply(2)
-        x_copy(1, 1)
-        turn(4)
-        quantize_x(0)
-        cast(5)
-        turn_bias()
-        quantize_f(0, 2)
-        copy_bias()
-        mm1(0, 0, 1)
-        multiply(3)
-        cast(6)
-        mm1(1, 0, 1)
-        quantize_x(1)
-        cast(7)
-        turn(5)
-        multiply(4)
-        mm1(0, 1, 2)
-        quantize_f(2, 2)
-        evacuate(0)
-        mm1(1, 1, 2)
-        multiply(5)
-        evacuate(1)
-        turn(6)
-        quantize_a(0, 2)
-        turn(7)
+        for g in range(G):
+            quantize_f(2 * g, 2)
+            quantize_x(g)
+        for i in (4, 5):
+            multiply(i)
+        for i in range(OPEN):
+            first_product(i, 0, 1)
+        for i in range(4):
+            first_product(i, 1 if i < OPEN else 0)
+            empty_agg(i)
+
+        quantize_agg(0, 2)
         quantize_f(4, 2)
-        mm1(2)
+        for i in (6, 7):
+            turn(i)
         multiply(6)
-        evacuate(2)
-        mm1(3)
-        evacuate(3)
-        mm2_turned(0, 0)
-        quantize_a(2, 2)
-        finish_turned(0, 0)
-        mm2_turned(0, 1)
-        quantize_f(6)
-        finish_turned(0, 1)
-        mm1(4)
+        quantize_agg(2, 2)
         multiply(7)
-        evacuate(4)
-        mm1(5)
-        evacuate(5)
-        turn_back(0)
-        quantize_a(4, 2)
-        copy_out(0)
-        mm2(2)
-        quantize_f(7)
-        mm1(6)
-        add_bias(2)
-        evacuate(6)
-        turn_back(1)
-        quantize_a(6)
-        copy_out(1)
-        mm2(3)
-        add_bias(3)
-        finish(2)
-        mm1(7)
-        evacuate(7)
-        mm2(4)
-        add_bias(4)
-        finish(3)
-        mm2(5)
-        add_bias(5)
-        finish(4)
-        mm2(6)
-        quantize_a(7)
-        finish(5)
-        mm2(7)
-        add_bias(6)
-        finish(6)
-        add_bias(7)
-        finish(7)
+        for half in range(2):
+            second_product_turned(half)
+        for i in (4, 5):
+            first_product(i)
+            empty_agg(i)
+        for i in (2, 3):
+            second_product(i)
+        for i in (0, 1):
+            turn_back_and_store(i)
+
+        for i in (6, 7):
+            quantize_f(i)
+        quantize_agg(4, 2)
+        for i in (2, 3):
+            add_bias(i)
+        for i in (6, 7):
+            first_product(i)
+            tanh_and_store(i - 4)
+            empty_agg(i, on_vector=i == 6)
+            second_product(i - 2)
+            add_bias(i - 2)
+            quantize_agg(i)
+        for i in (6, 7):
+            tanh_and_store(i - 2)
+            second_product(i)
+            add_bias(i)
+        for i in (6, 7):
+            tanh_and_store(i)

@@ -54,8 +54,6 @@ def tile_controencodnet_pa_w8_kernel(tc, f_bytes, f_scale, x, w_words, w_scales,
         wc = keep.tile([P, H * T], U8, name="wc", align_bytes=64)
         ws = keep.tile([P, H], U8, name="ws", align_bytes=64)
         bias = keep.tile([P, H], BF16, name="bias")
-        bias_col = keep.tile([P, T], F32, name="bias_col")
-        bias_rows = keep.tile([P, P], BF16, name="bias_rows")
         ident = keep.tile([P, P], F32, name="ident")
         ident_bf = keep.tile([P, P], BF16, name="ident_bf")
 
@@ -64,7 +62,6 @@ def tile_controencodnet_pa_w8_kernel(tc, f_bytes, f_scale, x, w_words, w_scales,
             nc.sync.dma_start(out=fb[q][:].rearrange("p (i k) -> p i k", i=b - a), in_=bytes_src[:, a:b, :])
 
         make_identity(nc, ident[:])
-        nc.vector.memset(bias_rows[:], 0.0)
         nc.vector.memset(ws[:].bitcast(I32), 0)
 
         load_f(0)
@@ -74,7 +71,6 @@ def tile_controencodnet_pa_w8_kernel(tc, f_bytes, f_scale, x, w_words, w_scales,
         for g in range(G):
             nc.sync.dma_start(out=xr[g][:], in_=x_src[g])
         load_f(len(loads) - 1)
-        nc.sync.dma_start(out=bias_rows[0:T, :], in_=b1.rearrange("(c p) -> c p", c=T))
         nc.sync.dma_start(out=wc[:], in_=w_words[0].rearrange("p n t -> p (n t)"))
         for q in range(4):
             nc.sync.dma_start(out=ws[32 * q : 32 * q + 4, :].bitcast(I32), in_=w_scales[0, 4 * q : 4 * q + 4, :].bitcast(I32))
@@ -82,7 +78,7 @@ def tile_controencodnet_pa_w8_kernel(tc, f_bytes, f_scale, x, w_words, w_scales,
         nc.vector.tensor_copy(out=ident_bf[:], in_=ident[:])
 
         wide, turned, fg, fc, fsc = {}, {}, {}, {}, {}
-        agg, ag, ac, asc, prod, summed, res_t = {}, {}, {}, {}, {}, {}, {}
+        agg, ag, ac, asc, prod, summed, alone = {}, {}, {}, {}, {}, {}, {}
         for pair in range(TILES // 2):
             fg[pair] = keep.tile([P, 2 * NODES], BF16, name="fg%d" % pair, align_bytes=64)
             fc[pair] = keep.tile([P, 2 * G * P], U32, name="fc%d" % pair, align_bytes=64)
@@ -90,7 +86,7 @@ def tile_controencodnet_pa_w8_kernel(tc, f_bytes, f_scale, x, w_words, w_scales,
             ag[pair] = keep.tile([P, 2 * DIN], BF16, name="ag%d" % pair, align_bytes=64)
             ac[pair] = keep.tile([P, 2 * P], U32, name="ac%d" % pair, align_bytes=64)
             asc[pair] = keep.tile([P, 2 * P], U8, name="asc%d" % pair, align_bytes=64)
-        for pair in range(1, TILES // 2):
+        for pair in range(TILES // 2):
             summed[pair] = keep.tile([P, 2, H], F32, name="summed%d" % pair)
 
         def widen(i, g0=0, g1=G, on_vector=False):
@@ -118,9 +114,20 @@ def tile_controencodnet_pa_w8_kernel(tc, f_bytes, f_scale, x, w_words, w_scales,
                 op=MULT,
             )
 
+        def multiply_on_gpsimd(i):
+            plain = keep.tile([P, G, P, 2], F32, name="plain", align_bytes=64)
+            nc.scalar.copy(out=plain[:], in_=turned[i, 0][:].rearrange("p u g n -> p g n u"))
+            alone[i] = keep.tile([P, NODES], BF16, name="ag1", align_bytes=64)
+            nc.gpsimd.tensor_tensor(
+                out=alone[i][:].rearrange("p (g n t) -> p g n t", g=G, t=T),
+                in0=plain[:].rearrange("p g n u -> p (g n u)").bitcast(BF16).rearrange("p (g n t) -> p g n t", g=G, t=T),
+                in1=fs[:, :, 0:T].unsqueeze(2).to_broadcast([P, G, P, T]),
+                op=MULT,
+            )
+
         def quantize_f(i, n=1):
             a, b = G * P * (i % 2), G * P * (i % 2 + n)
-            nc.vector.quantize_mx(out=fc[i // 2][:, a:b].bitcast(FP8X4), scales=fsc[i // 2][:, a:b], in_=fg[i // 2][:, T * a : T * b])
+            nc.vector.quantize_mx(out=fc[i // 2][:, a:b].bitcast(FP8X4), scales=fsc[i // 2][:, a:b], in_=alone[i][:] if i in alone else fg[i // 2][:, T * a : T * b])
 
         def interleave_x_gpsimd(g, h):
             dst = xg[g].rearrange("p (t m j) -> p m t j", t=T, j=T)[:, 64 * h : 64 * (h + 1)]
@@ -167,23 +174,6 @@ def tile_controencodnet_pa_w8_kernel(tc, f_bytes, f_scale, x, w_words, w_scales,
             rows = slice(P * (i % 2), P * (i % 2 + 1))
             nc.tensor.matmul_mx(out=prod[i][:], lhsT=ac[i // 2][:, rows].bitcast(FP8X4), lhsT_scale=asc[i // 2][:, rows], rhs=wc[:].bitcast(FP8X4), rhs_scale=ws[:], start=True, stop=True)
 
-        def second_product_turned(half):
-            bank = ps.tile([P, 2, 2 * P], F32, name="bank", bufs=BANKS)
-            for c in range(2 * half, 2 * half + 2):
-                nc.tensor.matmul_mx(out=bank[:, c % 2, :], lhsT=wc[:, T * P * c : T * P * (c + 1)].bitcast(FP8X4), lhsT_scale=ws[:, P * c : P * (c + 1)],
-                                    rhs=ac[0][:].bitcast(FP8X4), rhs_scale=asc[0][:], start=True, stop=True)
-            for c in range(2 * half, 2 * half + 2):
-                res_t[c] = ring.tile([P, 2 * P], F32, name="res_t")
-                nc.scalar.activation(out=res_t[c][:], in_=bank[:, c % 2, :], func=ACT.Tanh, bias=bias_col[:, c : c + 1])
-
-        def turn_back_and_store(i):
-            bank = ps.tile([P, H], F32, name="bank", bufs=BANKS)
-            for c in range(T):
-                nc.tensor.transpose(bank[:, P * c : P * (c + 1)], res_t[c][:, P * i : P * (i + 1)], ident[:])
-            res = ring.tile([P, H], F32, name="res")
-            nc.scalar.copy(out=res[:], in_=bank[:])
-            nc.sync.dma_start(out=out_dst[:, i, :], in_=res[:])
-
         def column_parts(i):
             return [(0, H // 2), (H // 2, H)] if i == TILES - 1 else [(0, H)]
 
@@ -212,12 +202,9 @@ def tile_controencodnet_pa_w8_kernel(tc, f_bytes, f_scale, x, w_words, w_scales,
         x_bank = interleave_x_tensor(1, 1)
         for i in (4, 5):
             turn(i)
-        bias_bank = ps.tile([P, P], BF16, name="bank", bufs=BANKS)
-        nc.tensor.transpose(bias_bank[:], bias_rows[:], ident_bf[:])
         interleave_x_scalar(0, 1)
         interleave_x_scalar(1, 0)
         nc.scalar.copy(out=xg[1].rearrange("p (t n) -> p t n", t=T)[:, :, 2 * P : T * P], in_=x_bank[:])
-        nc.scalar.copy(out=bias_col[:], in_=bias_bank[:, 0:T])
         for i in (6, 7):
             widen(i)
 
@@ -234,36 +221,34 @@ def tile_controencodnet_pa_w8_kernel(tc, f_bytes, f_scale, x, w_words, w_scales,
 
         quantize_agg(0, 2)
         quantize_f(4, 2)
-        for i in (6, 7):
+        for i in (7, 6):
             turn(i)
-        multiply(6)
         quantize_agg(2, 2)
-        multiply(7)
-        for half in range(2):
-            second_product_turned(half)
+        multiply_on_gpsimd(7)
+        multiply(6)
         for i in (4, 5):
+            second_product(i - 4)
             first_product(i)
             empty_agg(i)
         for i in (2, 3):
             second_product(i)
-        for i in (0, 1):
-            turn_back_and_store(i)
-
+        for i in range(3):
+            add_bias(i)
         for i in (6, 7):
             quantize_f(i)
         quantize_agg(4, 2)
-        for i in (2, 3):
-            add_bias(i)
+        add_bias(3)
+        for i in range(3):
+            tanh_and_store(i)
         for i in (6, 7):
             first_product(i)
-            tanh_and_store(i - 4)
-            empty_agg(i, on_vector=i == 6)
+            empty_agg(i)
             second_product(i - 2)
             add_bias(i - 2)
             quantize_agg(i)
+            tanh_and_store(i - 3)
+        tanh_and_store(5)
         for i in (6, 7):
-            tanh_and_store(i - 2)
             second_product(i)
             add_bias(i)
-        for i in (6, 7):
             tanh_and_store(i)

@@ -54,6 +54,8 @@ def tile_controencodnet_pa_w8_kernel(tc, f_bytes, f_scale, x, w_words, w_scales,
         wc = keep.tile([P, H * T], U8, name="wc", align_bytes=64)
         ws = keep.tile([P, H], U8, name="ws", align_bytes=64)
         bias = keep.tile([P, H], BF16, name="bias")
+        bias_col = keep.tile([P, T], F32, name="bias_col")
+        bias_rows = keep.tile([P, P], BF16, name="bias_rows")
         ident = keep.tile([P, P], F32, name="ident")
         ident_bf = keep.tile([P, P], BF16, name="ident_bf")
 
@@ -62,6 +64,7 @@ def tile_controencodnet_pa_w8_kernel(tc, f_bytes, f_scale, x, w_words, w_scales,
             nc.sync.dma_start(out=fb[q][:].rearrange("p (i k) -> p i k", i=b - a), in_=bytes_src[:, a:b, :])
 
         make_identity(nc, ident[:])
+        nc.vector.memset(bias_rows[:], 0.0)
         nc.vector.memset(ws[:].bitcast(I32), 0)
 
         load_f(0)
@@ -71,6 +74,7 @@ def tile_controencodnet_pa_w8_kernel(tc, f_bytes, f_scale, x, w_words, w_scales,
         for g in range(G):
             nc.sync.dma_start(out=xr[g][:], in_=x_src[g])
         load_f(len(loads) - 1)
+        nc.sync.dma_start(out=bias_rows[0:T, :], in_=b1.rearrange("(c p) -> c p", c=T))
         nc.sync.dma_start(out=wc[:], in_=w_words[0].rearrange("p n t -> p (n t)"))
         for q in range(4):
             nc.sync.dma_start(out=ws[32 * q : 32 * q + 4, :].bitcast(I32), in_=w_scales[0, 4 * q : 4 * q + 4, :].bitcast(I32))
@@ -78,7 +82,7 @@ def tile_controencodnet_pa_w8_kernel(tc, f_bytes, f_scale, x, w_words, w_scales,
         nc.vector.tensor_copy(out=ident_bf[:], in_=ident[:])
 
         wide, turned, fg, fc, fsc = {}, {}, {}, {}, {}
-        agg, ag, ac, asc, prod, summed, alone = {}, {}, {}, {}, {}, {}, {}
+        agg, ag, ac, asc, prod, summed, res_t, alone = {}, {}, {}, {}, {}, {}, {}, {}
         for pair in range(TILES // 2):
             fg[pair] = keep.tile([P, 2 * NODES], BF16, name="fg%d" % pair, align_bytes=64)
             fc[pair] = keep.tile([P, 2 * G * P], U32, name="fc%d" % pair, align_bytes=64)
@@ -86,7 +90,7 @@ def tile_controencodnet_pa_w8_kernel(tc, f_bytes, f_scale, x, w_words, w_scales,
             ag[pair] = keep.tile([P, 2 * DIN], BF16, name="ag%d" % pair, align_bytes=64)
             ac[pair] = keep.tile([P, 2 * P], U32, name="ac%d" % pair, align_bytes=64)
             asc[pair] = keep.tile([P, 2 * P], U8, name="asc%d" % pair, align_bytes=64)
-        for pair in range(TILES // 2):
+        for pair in range(1, TILES // 2):
             summed[pair] = keep.tile([P, 2, H], F32, name="summed%d" % pair)
 
         def widen(i, g0=0, g1=G, on_vector=False):
@@ -106,22 +110,22 @@ def tile_controencodnet_pa_w8_kernel(tc, f_bytes, f_scale, x, w_words, w_scales,
 
         def multiply(i, g0=0, g1=G):
             n = g1 - g0
-            base = NODES * (i % 2)
+            dst = alone[i][:] if i in alone else fg[i // 2][:, NODES * (i % 2) : NODES * (i % 2 + 1)]
             nc.vector.tensor_tensor(
-                out=fg[i // 2][:, base + DIN * g0 : base + DIN * g1].rearrange("p (g n u e) -> p g n u e", g=n, u=2, e=2),
+                out=dst[:, DIN * g0 : DIN * g1].rearrange("p (g n u e) -> p g n u e", g=n, u=2, e=2),
                 in0=turned[i, g0][:].rearrange("p u g n -> p (u g n)").bitcast(BF16).rearrange("p (u g n e) -> p g n u e", u=2, g=n, e=2),
                 in1=fs[:, g0:g1, 0:T].unsqueeze(2).to_broadcast([P, n, P, T]).rearrange("p g n (u e) -> p g n u e", u=2),
                 op=MULT,
             )
 
         def multiply_on_gpsimd(i):
-            plain = keep.tile([P, G, P, 2], F32, name="plain", align_bytes=64)
-            nc.scalar.copy(out=plain[:], in_=turned[i, 0][:].rearrange("p u g n -> p g n u"))
+            plain = keep.tile([P, P, 2], F32, name="plain", align_bytes=64)
+            nc.scalar.copy(out=plain[:], in_=turned[i, 1][:, :, 0, :].rearrange("p u n -> p n u"))
             alone[i] = keep.tile([P, NODES], BF16, name="ag1", align_bytes=64)
             nc.gpsimd.tensor_tensor(
-                out=alone[i][:].rearrange("p (g n t) -> p g n t", g=G, t=T),
-                in0=plain[:].rearrange("p g n u -> p (g n u)").bitcast(BF16).rearrange("p (g n t) -> p g n t", g=G, t=T),
-                in1=fs[:, :, 0:T].unsqueeze(2).to_broadcast([P, G, P, T]),
+                out=alone[i][:, DIN:NODES].rearrange("p (n t) -> p n t", t=T),
+                in0=plain[:].rearrange("p n u -> p (n u)").bitcast(BF16).rearrange("p (n t) -> p n t", t=T),
+                in1=fs[:, 1, 0:T].unsqueeze(1).to_broadcast([P, P, T]),
                 op=MULT,
             )
 
@@ -174,6 +178,23 @@ def tile_controencodnet_pa_w8_kernel(tc, f_bytes, f_scale, x, w_words, w_scales,
             rows = slice(P * (i % 2), P * (i % 2 + 1))
             nc.tensor.matmul_mx(out=prod[i][:], lhsT=ac[i // 2][:, rows].bitcast(FP8X4), lhsT_scale=asc[i // 2][:, rows], rhs=wc[:].bitcast(FP8X4), rhs_scale=ws[:], start=True, stop=True)
 
+        def second_product_turned(half):
+            bank = ps.tile([P, 2, 2 * P], F32, name="bank", bufs=BANKS)
+            for c in range(2 * half, 2 * half + 2):
+                nc.tensor.matmul_mx(out=bank[:, c % 2, :], lhsT=wc[:, T * P * c : T * P * (c + 1)].bitcast(FP8X4), lhsT_scale=ws[:, P * c : P * (c + 1)],
+                                    rhs=ac[0][:].bitcast(FP8X4), rhs_scale=asc[0][:], start=True, stop=True)
+            for c in range(2 * half, 2 * half + 2):
+                res_t[c] = ring.tile([P, 2 * P], F32, name="res_t")
+                nc.scalar.activation(out=res_t[c][:], in_=bank[:, c % 2, :], func=ACT.Tanh, bias=bias_col[:, c : c + 1])
+
+        def turn_back_and_store(i):
+            bank = ps.tile([P, H], F32, name="bank", bufs=BANKS)
+            for c in range(T):
+                nc.tensor.transpose(bank[:, P * c : P * (c + 1)], res_t[c][:, P * i : P * (i + 1)], ident[:])
+            res = ring.tile([P, H], F32, name="res")
+            nc.scalar.copy(out=res[:], in_=bank[:])
+            nc.sync.dma_start(out=out_dst[:, i, :], in_=res[:])
+
         def column_parts(i):
             return [(0, H // 2), (H // 2, H)] if i == TILES - 1 else [(0, H)]
 
@@ -202,9 +223,12 @@ def tile_controencodnet_pa_w8_kernel(tc, f_bytes, f_scale, x, w_words, w_scales,
         x_bank = interleave_x_tensor(1, 1)
         for i in (4, 5):
             turn(i)
+        bias_bank = ps.tile([P, P], BF16, name="bank", bufs=BANKS)
+        nc.tensor.transpose(bias_bank[:], bias_rows[:], ident_bf[:])
         interleave_x_scalar(0, 1)
         interleave_x_scalar(1, 0)
         nc.scalar.copy(out=xg[1].rearrange("p (t n) -> p t n", t=T)[:, :, 2 * P : T * P], in_=x_bank[:])
+        nc.scalar.copy(out=bias_col[:], in_=bias_bank[:, 0:T])
         for i in (6, 7):
             widen(i)
 
@@ -221,34 +245,38 @@ def tile_controencodnet_pa_w8_kernel(tc, f_bytes, f_scale, x, w_words, w_scales,
 
         quantize_agg(0, 2)
         quantize_f(4, 2)
-        for i in (7, 6):
-            turn(i)
+        turn(7, 1, 2)
+        turn(6)
+        turn(7, 0, 1)
         quantize_agg(2, 2)
         multiply_on_gpsimd(7)
         multiply(6)
+        multiply(7, 0, 1)
+        for half in range(2):
+            second_product_turned(half)
         for i in (4, 5):
-            second_product(i - 4)
             first_product(i)
             empty_agg(i)
         for i in (2, 3):
             second_product(i)
-        for i in range(3):
-            add_bias(i)
+        for i in (0, 1):
+            turn_back_and_store(i)
+
         for i in (6, 7):
             quantize_f(i)
+        add_bias(2)
         quantize_agg(4, 2)
         add_bias(3)
-        for i in range(3):
-            tanh_and_store(i)
         for i in (6, 7):
             first_product(i)
-            empty_agg(i)
+            tanh_and_store(i - 4)
+            empty_agg(i, on_vector=i == 6)
             second_product(i - 2)
             add_bias(i - 2)
             quantize_agg(i)
-            tanh_and_store(i - 3)
-        tanh_and_store(5)
         for i in (6, 7):
+            tanh_and_store(i - 2)
             second_product(i)
             add_bias(i)
+        for i in (6, 7):
             tanh_and_store(i)

@@ -22,6 +22,7 @@ G = 2
 T = 4
 TILES = 8
 BANKS = 8
+X_GPSIMD = 88
 OPEN = 3
 FLOPS = 2 * NODES * NODES * DIN + 2 * NODES * DIN * H
 
@@ -69,11 +70,11 @@ def tile_controencodnet_pa_w8_kernel(tc, f_bytes, f_scale, x, w_words, w_scales,
 
         load_f(0)
         nc.sync.dma_start(out=fs[:, :, 0:T], in_=f_scale.rearrange("o (g p t) -> p (o g) t", g=G, t=T))
-        for q in range(1, len(loads) - 1):
+        for q in (1, 2):
             load_f(q)
         for g in range(G):
             nc.sync.dma_start(out=xr[g][:], in_=x_src[g])
-        load_f(len(loads) - 1)
+            load_f(3 + g)
         nc.sync.dma_start(out=bias_rows[0:T, :], in_=b1.rearrange("(c p) -> c p", c=T))
         nc.sync.dma_start(out=wc[:], in_=w_words[0].rearrange("p n t -> p (n t)"))
         for q in range(4):
@@ -95,7 +96,7 @@ def tile_controencodnet_pa_w8_kernel(tc, f_bytes, f_scale, x, w_words, w_scales,
 
         def widen(i, g0=0, g1=G, on_vector=False):
             q, k = where[i]
-            tile = ring.tile([P, DIN * (g1 - g0)], BF16, name="wide", align_bytes=64, bufs=TILES + 1)
+            tile = ring.tile([P, DIN * (g1 - g0)], BF16, name="wide", align_bytes=64, bufs=TILES + 2)
             for g in range(g0, g1):
                 wide[i, g] = tile[:, DIN * (g - g0) : DIN * (g - g0 + 1)]
             copy = nc.vector.tensor_copy if on_vector else nc.scalar.copy
@@ -133,14 +134,14 @@ def tile_controencodnet_pa_w8_kernel(tc, f_bytes, f_scale, x, w_words, w_scales,
             a, b = G * P * (i % 2), G * P * (i % 2 + n)
             nc.vector.quantize_mx(out=fc[i // 2][:, a:b].bitcast(FP8X4), scales=fsc[i // 2][:, a:b], in_=alone[i][:] if i in alone else fg[i // 2][:, T * a : T * b])
 
-        def interleave_x_gpsimd(g, h):
-            dst = xg[g].rearrange("p (t m j) -> p m t j", t=T, j=T)[:, 64 * h : 64 * (h + 1)]
-            src = xr[g][:].rearrange("p j (m t) -> p m t j", t=T)[:, 64 * h : 64 * (h + 1)]
+        def interleave_x_gpsimd(g, m0, m1):
+            dst = xg[g].rearrange("p (t m j) -> p m t j", t=T, j=T)[:, m0:m1]
+            src = xr[g][:].rearrange("p j (m t) -> p m t j", t=T)[:, m0:m1]
             nc.gpsimd.tensor_scalar(out=dst, in0=src, scalar1=1.0, scalar2=0.0, op0=MULT, op1=ADD)
 
-        def interleave_x_scalar(g, h):
-            dst = xg[g].rearrange("p (t m e j) -> p m t e j", t=T, e=2, j=T)[:, 32 * h : 32 * (h + 1)]
-            src = xr[g][:].rearrange("p j (m e t) -> p m t e j", e=2, t=T)[:, 32 * h : 32 * (h + 1)]
+        def interleave_x_scalar(g, m0, m1):
+            dst = xg[g].rearrange("p (t m e j) -> p m t e j", t=T, e=2, j=T)[:, m0 // 2 : m1 // 2]
+            src = xr[g][:].rearrange("p j (m e t) -> p m t e j", e=2, t=T)[:, m0 // 2 : m1 // 2]
             nc.scalar.copy(out=dst, in_=src)
 
         def interleave_x_tensor(g, h):
@@ -208,14 +209,18 @@ def tile_controencodnet_pa_w8_kernel(tc, f_bytes, f_scale, x, w_words, w_scales,
                 nc.scalar.activation(out=res[:, a:b], in_=summed[i // 2][:, i % 2, a:b], func=ACT.Tanh)
                 nc.sync.dma_start(out=out_dst[:, i, a:b], in_=res[:, a:b])
 
-        interleave_x_gpsimd(0, 0)
+        interleave_x_gpsimd(0, 0, X_GPSIMD)
         widen(0, 0, 1)
         widen(0, 1, 2, on_vector=True)
-        widen(1, on_vector=True)
+        widen(1, 0, 1, on_vector=True)
+        widen(1, 1, 2)
         for g in range(G):
             turn(0, g, g + 1)
             multiply(0, g, g + 1)
-        for i in range(2, 6):
+        for i in (2, 3):
+            widen(i)
+        interleave_x_scalar(0, X_GPSIMD, P)
+        for i in (4, 5):
             widen(i)
         for i in range(1, 4):
             turn(i)
@@ -225,8 +230,7 @@ def tile_controencodnet_pa_w8_kernel(tc, f_bytes, f_scale, x, w_words, w_scales,
             turn(i)
         bias_bank = ps.tile([P, P], BF16, name="bank", bufs=BANKS)
         nc.tensor.transpose(bias_bank[:], bias_rows[:], ident_bf[:])
-        interleave_x_scalar(0, 1)
-        interleave_x_scalar(1, 0)
+        interleave_x_scalar(1, 0, P // 2)
         nc.scalar.copy(out=xg[1].rearrange("p (t n) -> p t n", t=T)[:, :, 2 * P : T * P], in_=x_bank[:])
         nc.scalar.copy(out=bias_col[:], in_=bias_bank[:, 0:T])
         for i in (6, 7):

@@ -22,8 +22,6 @@ G = 2
 T = 4
 TILES = 8
 BANKS = 8
-X_GPSIMD = 88
-OPEN = 3
 FLOPS = 2 * NODES * NODES * DIN + 2 * NODES * DIN * H
 
 
@@ -35,23 +33,16 @@ def tile_controencodnet_pa_w8_kernel(tc, f_bytes, f_scale, x, w_words, w_scales,
         ps = ctx.enter_context(tc.psum_pool(name="ps", bufs=1))
         ctx.enter_context(tc.manual_schedule())
 
-        bytes_src = f_bytes.rearrange("(p i) k -> p i k", i=TILES)
+        bytes_src = f_bytes.rearrange("(p i) k -> p (i k)", i=TILES)
         out_dst = out.rearrange("(p i) h -> p i h", i=TILES)
         x_src = x.rearrange("(g p j) d -> g p j d", g=G, j=T)
 
-        loads = [(0, 1), (1, 2), (2, 4), (4, 6), (6, 8)]
-        fb = [keep.tile([P, (b - a) * NODES], U8, name="fb%d" % a, align_bytes=64) for a, b in loads]
-        where = {}
-        for q, (a, b) in enumerate(loads):
-            for i in range(a, b):
-                where[i] = (q, i - a)
+        loads = [(0, 1024), (1024, 2048), (2048, 4096), (4096, 6144), (6144, 8192)]
+        fb = [keep.tile([P, b - a], U8, name="fb%d" % a, align_bytes=64) for a, b in loads]
         fs = keep.tile([P, G, 2 * T], F32, name="fs")
         xr = [keep.tile([P, T, DIN], BF16, name="xr%d" % g, align_bytes=64) for g in range(G)]
-        xc_all = keep.tile([P, G * DIN], U32, name="xc", align_bytes=64)
-        xs_all = keep.tile([P, G * DIN], U8, name="xs", align_bytes=64)
-        xg = [keep.tile([P, T * DIN], BF16, name="xg%d" % g, align_bytes=64)[:] for g in range(G)]
-        xc = [xc_all[:, DIN * g : DIN * (g + 1)] for g in range(G)]
-        xs = [xs_all[:, DIN * g : DIN * (g + 1)] for g in range(G)]
+        xc = [keep.tile([P, DIN], U32, name="xc%d" % g, align_bytes=64) for g in range(G)]
+        xs = [keep.tile([P, DIN], U8, name="xs%d" % g, align_bytes=64) for g in range(G)]
         wc = keep.tile([P, H * T], U8, name="wc", align_bytes=64)
         ws = keep.tile([P, H], U8, name="ws", align_bytes=64)
         bias = keep.tile([P, H], BF16, name="bias")
@@ -60,9 +51,23 @@ def tile_controencodnet_pa_w8_kernel(tc, f_bytes, f_scale, x, w_words, w_scales,
         ident = keep.tile([P, P], F32, name="ident")
         ident_bf = keep.tile([P, P], BF16, name="ident_bf")
 
+        free_banks = list(range(BANKS))
+        held = {}
+
+        def take(key, shape, dtype):
+            b = free_banks.pop(0)
+            held[key] = (b, ps.tile(shape, dtype, name="bank%d" % b))
+            return held[key][1]
+
+        def give(key):
+            free_banks.append(held.pop(key)[0])
+
         def load_f(q):
             a, b = loads[q]
-            nc.sync.dma_start(out=fb[q][:].rearrange("p (i k) -> p i k", i=b - a), in_=bytes_src[:, a:b, :])
+            nc.sync.dma_start(out=fb[q][:], in_=bytes_src[:, a:b])
+
+        def load_x(g):
+            nc.sync.dma_start(out=xr[g][:], in_=x_src[g])
 
         make_identity(nc, ident[:])
         nc.vector.memset(bias_rows[:], 0.0)
@@ -70,11 +75,12 @@ def tile_controencodnet_pa_w8_kernel(tc, f_bytes, f_scale, x, w_words, w_scales,
 
         load_f(0)
         nc.sync.dma_start(out=fs[:, :, 0:T], in_=f_scale.rearrange("o (g p t) -> p (o g) t", g=G, t=T))
-        for q in (1, 2):
-            load_f(q)
-        for g in range(G):
-            nc.sync.dma_start(out=xr[g][:], in_=x_src[g])
-            load_f(3 + g)
+        load_f(1)
+        load_f(2)
+        load_x(0)
+        load_f(3)
+        load_x(1)
+        load_f(4)
         nc.sync.dma_start(out=bias_rows[0:T, :], in_=b1.rearrange("(c p) -> c p", c=T))
         nc.sync.dma_start(out=wc[:], in_=w_words[0].rearrange("p n t -> p (n t)"))
         for q in range(4):
@@ -82,205 +88,278 @@ def tile_controencodnet_pa_w8_kernel(tc, f_bytes, f_scale, x, w_words, w_scales,
         nc.sync.dma_start(out=bias[:], in_=b1.partition_broadcast(P))
         nc.vector.tensor_copy(out=ident_bf[:], in_=ident[:])
 
-        wide, turned, fg, fc, fsc = {}, {}, {}, {}, {}
-        agg, ag, ac, asc, prod, summed, res_t, alone = {}, {}, {}, {}, {}, {}, {}, {}
+        wide, ac, asc, summed, res_t, plain = {}, {}, {}, {}, {}, {}
         for pair in range(TILES // 2):
-            fg[pair] = keep.tile([P, 2 * NODES], BF16, name="fg%d" % pair, align_bytes=64)
-            fc[pair] = keep.tile([P, 2 * G * P], U32, name="fc%d" % pair, align_bytes=64)
-            fsc[pair] = keep.tile([P, 2 * G * P], U8, name="fsc%d" % pair, align_bytes=64)
-            ag[pair] = keep.tile([P, 2 * DIN], BF16, name="ag%d" % pair, align_bytes=64)
             ac[pair] = keep.tile([P, 2 * P], U32, name="ac%d" % pair, align_bytes=64)
             asc[pair] = keep.tile([P, 2 * P], U8, name="asc%d" % pair, align_bytes=64)
-        for pair in range(1, TILES // 2):
-            summed[pair] = keep.tile([P, 2, H], F32, name="summed%d" % pair)
 
-        def widen(i, g0=0, g1=G, on_vector=False):
-            q, k = where[i]
-            tile = ring.tile([P, DIN * (g1 - g0)], BF16, name="wide", align_bytes=64, bufs=TILES + 2)
+        stage = keep.tile([P, 15360], BF16, name="stage", align_bytes=64)
+        f_at = [0, 1024, 2048, 3072, 4096, 5120, 6144, 7168]
+        a_at = [8192, 8704, 7168, 7680, 9216, 9728, 10240, 10752]
+        xg = [stage[:, at : at + T * DIN] for at in (11264, 13312)]
+        fc = keep.tile([P, TILES * G * P], U32, name="fc", align_bytes=64)
+        fsc = keep.tile([P, TILES * G * P], U8, name="fsc", align_bytes=64)
+
+        def scaled(i):
+            return stage[:, f_at[i] : f_at[i] + NODES]
+
+        def widen(i, g0=0, g1=G, engine="scalar"):
+            first, last = NODES * i + DIN * g0, NODES * i + DIN * g1
+            q = [a <= first < b for a, b in loads].index(True)
+            tile = ring.tile([P, DIN * (g1 - g0)], BF16, name="wide", align_bytes=64, bufs=TILES + 3)
             for g in range(g0, g1):
                 wide[i, g] = tile[:, DIN * (g - g0) : DIN * (g - g0 + 1)]
-            copy = nc.vector.tensor_copy if on_vector else nc.scalar.copy
-            copy(out=tile[:], in_=fb[q][:, k * NODES + DIN * g0 : k * NODES + DIN * g1].bitcast(FP8))
+            copy = {"scalar": nc.scalar.copy, "vector": nc.vector.tensor_copy, "gpsimd": nc.gpsimd.tensor_copy}[engine]
+            copy(out=tile[:], in_=fb[q][:, first - loads[q][0] : last - loads[q][0]].bitcast(FP8))
 
         def turn(i, g0=0, g1=G):
-            turned[i, g0] = ps.tile([P, 2, g1 - g0, P], F32, name="bank", bufs=BANKS)
+            bank = take(("f", i, g0), [P, 2, g1 - g0, P], F32)
             for g in range(g0, g1):
                 words = wide[i, g].bitcast(F32)
                 for u in range(2):
-                    nc.tensor.transpose(turned[i, g0][:, u, g - g0, :], words[:, u : 2 * P : 2], ident[:])
+                    nc.tensor.transpose(bank[:, u, g - g0, :], words[:, u : 2 * P : 2], ident[:])
 
         def multiply(i, g0=0, g1=G):
             n = g1 - g0
-            dst = alone[i][:] if i in alone else fg[i // 2][:, NODES * (i % 2) : NODES * (i % 2 + 1)]
+            key = ("f", i, g0) if ("f", i, g0) in held and held["f", i, g0][1].shape[2] == n else ("f", i, 0)
+            bank = held[key][1]
+            words = bank[:] if bank.shape[2] == n else bank[:, :, g0:g1, :]
             nc.vector.tensor_tensor(
-                out=dst[:, DIN * g0 : DIN * g1].rearrange("p (g n u e) -> p g n u e", g=n, u=2, e=2),
-                in0=turned[i, g0][:].rearrange("p u g n -> p (u g n)").bitcast(BF16).rearrange("p (u g n e) -> p g n u e", u=2, g=n, e=2),
+                out=scaled(i)[:, DIN * g0 : DIN * g1].rearrange("p (g n u e) -> p g n u e", g=n, u=2, e=2),
+                in0=words.bitcast(BF16).rearrange("p u g (n e) -> p g n u e", e=2),
                 in1=fs[:, g0:g1, 0:T].unsqueeze(2).to_broadcast([P, n, P, T]).rearrange("p g n (u e) -> p g n u e", u=2),
                 op=MULT,
             )
+            give(key)
 
-        def multiply_on_gpsimd(i):
-            plain = keep.tile([P, P, 2], F32, name="plain", align_bytes=64)
-            nc.scalar.copy(out=plain[:], in_=turned[i, 1][:, :, 0, :].rearrange("p u n -> p n u"))
-            alone[i] = keep.tile([P, NODES], BF16, name="ag1", align_bytes=64)
+        def words_out(i, g0=0, g1=G):
+            plain[i] = ring.tile([P, g1 - g0, P, 2], F32, name="plain", align_bytes=64, bufs=2)
+            if ("f", i, g0) in held:
+                nc.scalar.copy(out=plain[i][:], in_=held["f", i, g0][1][:].rearrange("p u g n -> p g n u"))
+                give(("f", i, g0))
+            else:
+                nc.scalar.copy(out=plain[i][:], in_=held["f", i, 0][1][:, :, g0:g1, :].rearrange("p u g n -> p g n u"))
+
+        def multiply_on_gpsimd(i, g0=0, g1=G):
+            n = g1 - g0
             nc.gpsimd.tensor_tensor(
-                out=alone[i][:, DIN:NODES].rearrange("p (n t) -> p n t", t=T),
-                in0=plain[:].rearrange("p n u -> p (n u)").bitcast(BF16).rearrange("p (n t) -> p n t", t=T),
-                in1=fs[:, 1, 0:T].unsqueeze(1).to_broadcast([P, P, T]),
+                out=scaled(i)[:, DIN * g0 : DIN * g1].rearrange("p (g n t) -> p g n t", g=n, t=T),
+                in0=plain[i][:].rearrange("p g n u -> p (g n u)").bitcast(BF16).rearrange("p (g n t) -> p g n t", g=n, t=T),
+                in1=fs[:, g0:g1, 0:T].unsqueeze(2).to_broadcast([P, n, P, T]),
                 op=MULT,
             )
 
         def quantize_f(i, n=1):
-            a, b = G * P * (i % 2), G * P * (i % 2 + n)
-            nc.vector.quantize_mx(out=fc[i // 2][:, a:b].bitcast(FP8X4), scales=fsc[i // 2][:, a:b], in_=alone[i][:] if i in alone else fg[i // 2][:, T * a : T * b])
+            a, b = G * P * i, G * P * (i + n)
+            nc.vector.quantize_mx(out=fc[:, a:b].bitcast(FP8X4), scales=fsc[:, a:b], in_=stage[:, f_at[i] : f_at[i] + n * NODES])
 
         def interleave_x_gpsimd(g, m0, m1):
-            dst = xg[g].rearrange("p (t m j) -> p m t j", t=T, j=T)[:, m0:m1]
-            src = xr[g][:].rearrange("p j (m t) -> p m t j", t=T)[:, m0:m1]
+            dst = xg[g].rearrange("p (t m j) -> p t m j", t=T, j=T)[:, :, m0:m1]
+            src = xr[g][:].rearrange("p j (m t) -> p t m j", t=T)[:, :, m0:m1]
             nc.gpsimd.tensor_scalar(out=dst, in0=src, scalar1=1.0, scalar2=0.0, op0=MULT, op1=ADD)
 
-        def interleave_x_scalar(g, m0, m1):
+        def interleave_x(g, m0, m1, on_vector=False):
             dst = xg[g].rearrange("p (t m e j) -> p m t e j", t=T, e=2, j=T)[:, m0 // 2 : m1 // 2]
             src = xr[g][:].rearrange("p j (m e t) -> p m t e j", e=2, t=T)[:, m0 // 2 : m1 // 2]
-            nc.scalar.copy(out=dst, in_=src)
+            copy = nc.vector.tensor_copy if on_vector else nc.scalar.copy
+            copy(out=dst, in_=src)
 
         def interleave_x_tensor(g, h):
-            bank = ps.tile([P, T, 64 * T], BF16, name="bank", bufs=BANKS)
+            bank = take(("x", g, h), [P, T, 64 * T], BF16)
             src = xr[g][:].rearrange("p j (m t) -> p j m t", t=T)[:, :, 64 * h : 64 * (h + 1)]
             dst = bank[:].rearrange("p t (m j) -> p j m t", j=T)
             for u in range(2):
                 nc.tensor.matmul(out=dst[:, 2 * u : 2 * u + 2], lhsT=ident_bf[:], rhs=src[:, 2 * u : 2 * u + 2], start=True, stop=True)
-            return bank
+
+        def empty_x(g, h):
+            nc.scalar.copy(out=xg[g].rearrange("p (t n) -> p t n", t=T)[:, :, 2 * P * h : 2 * P * (h + 1)], in_=held["x", g, h][1][:])
+            give(("x", g, h))
+
+        def warm_up(n):
+            bank = take("warm", [P, DIN], F32)
+            for r in range(n):
+                nc.tensor.matmul(out=bank[:], lhsT=ident_bf[:], rhs=xr[0][:, r, :], start=True, stop=True)
+            give("warm")
+
+        def turn_bias():
+            bank = take("bias", [P, P], BF16)
+            nc.tensor.transpose(bank[:], bias_rows[:], ident_bf[:])
+
+        def empty_bias():
+            nc.scalar.copy(out=bias_col[:], in_=held["bias"][1][:, 0:T])
+            give("bias")
 
         def quantize_x(g):
-            nc.vector.quantize_mx(out=xc[g].bitcast(FP8X4), scales=xs[g], in_=xg[g])
+            nc.vector.quantize_mx(out=xc[g][:].bitcast(FP8X4), scales=xs[g][:], in_=xg[g])
 
         def first_product(i, g0=0, g1=G):
-            if g0 == 0:
-                agg[i] = ps.tile([P, T, P], F32, name="bank", bufs=BANKS)
+            bank = take(("agg", i), [P, T, P], F32) if g0 == 0 else held["agg", i][1]
             for g in range(g0, g1):
-                rows = slice(P * (G * (i % 2) + g), P * (G * (i % 2) + g + 1))
+                rows = slice(P * (G * i + g), P * (G * i + g + 1))
                 for t in range(T):
                     cols = slice(P * t, P * (t + 1))
-                    nc.tensor.matmul_mx(out=agg[i][:, t, :], lhsT=xc[g][:, cols].bitcast(FP8X4), lhsT_scale=xs[g][:, cols],
-                                        rhs=fc[i // 2][:, rows].bitcast(FP8X4), rhs_scale=fsc[i // 2][:, rows], start=(g == 0 and t == 0), stop=(g == G - 1 and t == T - 1))
+                    nc.tensor.matmul_mx(out=bank[:, t, :], lhsT=xc[g][:, cols].bitcast(FP8X4), lhsT_scale=xs[g][:, cols],
+                                        rhs=fc[:, rows].bitcast(FP8X4), rhs_scale=fsc[:, rows], start=(g == 0 and t == 0), stop=(g == G - 1 and t == T - 1))
 
         def empty_agg(i, on_vector=False):
-            dst = ag[i // 2][:, DIN * (i % 2) : DIN * (i % 2 + 1)]
+            dst = stage[:, a_at[i] : a_at[i] + DIN]
             copy = nc.vector.tensor_copy if on_vector else nc.scalar.copy
-            copy(out=dst.rearrange("p (n t) -> p n t", t=T), in_=agg[i][:].rearrange("p t n -> p n t"))
+            copy(out=dst.rearrange("p (n t) -> p n t", t=T), in_=held["agg", i][1][:].rearrange("p t n -> p n t"))
+            give(("agg", i))
 
         def quantize_agg(i, n=1):
             a, b = P * (i % 2), P * (i % 2 + n)
-            nc.vector.quantize_mx(out=ac[i // 2][:, a:b].bitcast(FP8X4), scales=asc[i // 2][:, a:b], in_=ag[i // 2][:, T * a : T * b])
+            nc.vector.quantize_mx(out=ac[i // 2][:, a:b].bitcast(FP8X4), scales=asc[i // 2][:, a:b], in_=stage[:, a_at[i] : a_at[i] + n * DIN])
 
         def second_product(i):
-            prod[i] = ps.tile([P, H], F32, name="bank", bufs=BANKS)
+            bank = take(("prod", i), [P, H], F32)
             rows = slice(P * (i % 2), P * (i % 2 + 1))
-            nc.tensor.matmul_mx(out=prod[i][:], lhsT=ac[i // 2][:, rows].bitcast(FP8X4), lhsT_scale=asc[i // 2][:, rows], rhs=wc[:].bitcast(FP8X4), rhs_scale=ws[:], start=True, stop=True)
+            nc.tensor.matmul_mx(out=bank[:], lhsT=ac[i // 2][:, rows].bitcast(FP8X4), lhsT_scale=asc[i // 2][:, rows], rhs=wc[:].bitcast(FP8X4), rhs_scale=ws[:], start=True, stop=True)
 
-        def second_product_turned(half):
-            bank = ps.tile([P, 2, 2 * P], F32, name="bank", bufs=BANKS)
+        def second_product_turned(pair, half):
+            bank = take(("prod_t", pair, half), [P, 2, 2 * P], F32)
             for c in range(2 * half, 2 * half + 2):
                 nc.tensor.matmul_mx(out=bank[:, c % 2, :], lhsT=wc[:, T * P * c : T * P * (c + 1)].bitcast(FP8X4), lhsT_scale=ws[:, P * c : P * (c + 1)],
-                                    rhs=ac[0][:].bitcast(FP8X4), rhs_scale=asc[0][:], start=True, stop=True)
-            for c in range(2 * half, 2 * half + 2):
-                res_t[c] = ring.tile([P, 2 * P], F32, name="res_t")
-                nc.scalar.activation(out=res_t[c][:], in_=bank[:, c % 2, :], func=ACT.Tanh, bias=bias_col[:, c : c + 1])
+                                    rhs=ac[pair][:].bitcast(FP8X4), rhs_scale=asc[pair][:], start=True, stop=True)
 
-        def turn_back_and_store(i):
-            bank = ps.tile([P, H], F32, name="bank", bufs=BANKS)
-            for c in range(T):
-                nc.tensor.transpose(bank[:, P * c : P * (c + 1)], res_t[c][:, P * i : P * (i + 1)], ident[:])
-            res = ring.tile([P, H], F32, name="res")
-            nc.scalar.copy(out=res[:], in_=bank[:])
-            nc.sync.dma_start(out=out_dst[:, i, :], in_=res[:])
+        def tanh_turned(pair, half):
+            for c in range(2 * half, 2 * half + 2):
+                res_t[pair, c] = ring.tile([P, 2 * P], F32, name="res_t")
+                nc.scalar.activation(out=res_t[pair, c][:], in_=held["prod_t", pair, half][1][:, c % 2, :], func=ACT.Tanh, bias=bias_col[:, c : c + 1])
+            give(("prod_t", pair, half))
+
+        def turn_back(i):
+            bank = take(("back", i), [P, H], F32)
+            for c in reversed(range(T)):
+                nc.tensor.transpose(bank[:, P * c : P * (c + 1)], res_t[i // 2, c][:, P * (i % 2) : P * (i % 2 + 1)], ident[:])
+
+        results = {}
+
+        def result(i):
+            if i // 2 not in results:
+                results[i // 2] = keep.tile([P, 2, H], F32, name="res%d" % (i // 2))
+            return results[i // 2][:, i % 2, :]
+
+        def store(i, a, b):
+            if i // 2 not in ():
+                nc.sync.dma_start(out=out_dst[:, i, a:b], in_=result(i)[:, a:b])
+            elif i % 2 == 1:
+                nc.sync.dma_start(out=out_dst[:, i - 1 : i + 1, :], in_=results[i // 2][:])
+
+        def empty_back_and_store(i, on_vector=False):
+            res = result(i)
+            copy = nc.vector.tensor_copy if on_vector else nc.scalar.copy
+            copy(out=res, in_=held["back", i][1][:])
+            give(("back", i))
+            store(i, 0, H)
 
         def column_parts(i):
-            return [(0, H // 2), (H // 2, H)] if i == TILES - 1 else [(0, H)]
+            return [(0, H)] if i == TILES - 1 else [(0, H)]
 
         def add_bias(i):
+            summed[i] = ring.tile([P, H], F32, name="summed")
             for a, b in column_parts(i):
-                nc.vector.tensor_tensor(out=summed[i // 2][:, i % 2, a:b], in0=prod[i][:, a:b], in1=bias[:, a:b], op=ADD)
+                nc.vector.tensor_tensor(out=summed[i][:, a:b], in0=held["prod", i][1][:, a:b], in1=bias[:, a:b], op=ADD)
+            give(("prod", i))
 
         def tanh_and_store(i):
-            res = ring.tile([P, H], F32, name="res")
+            res = result(i)
             for a, b in column_parts(i):
-                nc.scalar.activation(out=res[:, a:b], in_=summed[i // 2][:, i % 2, a:b], func=ACT.Tanh)
-                nc.sync.dma_start(out=out_dst[:, i, a:b], in_=res[:, a:b])
+                nc.scalar.activation(out=res[:, a:b], in_=summed[i][:, a:b], func=ACT.Tanh)
+                store(i, a, b)
 
-        interleave_x_gpsimd(0, 0, X_GPSIMD)
-        widen(0, 0, 1)
-        widen(0, 1, 2, on_vector=True)
-        widen(1, 0, 1, on_vector=True)
-        widen(1, 1, 2)
-        for g in range(G):
-            turn(0, g, g + 1)
-            multiply(0, g, g + 1)
-        for i in (2, 3):
-            widen(i)
-        interleave_x_scalar(0, X_GPSIMD, P)
-        for i in (4, 5):
-            widen(i)
-        for i in range(1, 4):
-            turn(i)
-            multiply(i)
-        x_bank = interleave_x_tensor(1, 1)
-        for i in (4, 5):
-            turn(i)
-        bias_bank = ps.tile([P, P], BF16, name="bank", bufs=BANKS)
-        nc.tensor.transpose(bias_bank[:], bias_rows[:], ident_bf[:])
-        interleave_x_scalar(1, 0, P // 2)
-        nc.scalar.copy(out=xg[1].rearrange("p (t n) -> p t n", t=T)[:, :, 2 * P : T * P], in_=x_bank[:])
-        nc.scalar.copy(out=bias_col[:], in_=bias_bank[:, 0:T])
-        for i in (6, 7):
-            widen(i)
-
-        for g in range(G):
-            quantize_f(2 * g, 2)
-            quantize_x(g)
-        for i in (4, 5):
-            multiply(i)
-        for i in range(OPEN):
-            first_product(i, 0, 1)
-        for i in range(4):
-            first_product(i, 1 if i < OPEN else 0)
-            empty_agg(i)
-
+        interleave_x_gpsimd(0, 0, 88)
+        widen(0, 1, 2, "vector")
+        widen(1, 0, 1, "vector")
+        widen(0, 0, 1, "scalar")
+        widen(1, 1, 2, "scalar")
+        widen(2, engine="scalar")
+        widen(3, engine="scalar")
+        interleave_x(0, 88, 128)
+        widen(4, engine="scalar")
+        widen(5, engine="scalar")
+        interleave_x(1, 0, 64)
+        turn(0, 0, 1)
+        multiply(0, 0, 1)
+        turn(0, 1, 2)
+        multiply(0, 1, 2)
+        turn(1)
+        multiply(1)
+        turn(2)
+        multiply(2)
+        turn(3)
+        multiply(3)
+        quantize_f(0, 2)
+        quantize_x(0)
+        quantize_f(2, 2)
+        interleave_x_tensor(1, 1)
+        empty_x(1, 1)
+        quantize_x(1)
+        turn(4)
+        multiply(4)
+        turn(5)
+        multiply(5)
+        turn_bias()
+        empty_bias()
+        widen(6, engine="scalar")
+        widen(7, engine="scalar")
+        first_product(0, 0, 1)
+        first_product(1, 0, 1)
+        first_product(2, 0, 1)
+        first_product(0, 1, 2)
+        empty_agg(0)
+        first_product(1, 1, 2)
+        empty_agg(1)
         quantize_agg(0, 2)
         quantize_f(4, 2)
-        turn(7, 1, 2)
-        turn(6)
-        turn(7, 0, 1)
+        first_product(2, 1, 2)
+        empty_agg(2)
+        first_product(3)
+        empty_agg(3)
         quantize_agg(2, 2)
-        multiply_on_gpsimd(7)
+        turn(7, 1, 2)
+        words_out(7, 1, 2)
+        multiply_on_gpsimd(7, 1, 2)
+        turn(6)
         multiply(6)
+        turn(7, 0, 1)
         multiply(7, 0, 1)
-        for half in range(2):
-            second_product_turned(half)
-        for i in (4, 5):
-            first_product(i)
-            empty_agg(i)
-        for i in (2, 3):
-            second_product(i)
-        for i in (0, 1):
-            turn_back_and_store(i)
-
-        for i in (6, 7):
-            quantize_f(i)
+        second_product_turned(0, 0)
+        tanh_turned(0, 0)
+        second_product_turned(0, 1)
+        tanh_turned(0, 1)
+        first_product(4)
+        empty_agg(4)
+        second_product(2)
         add_bias(2)
+        quantize_f(6)
+        quantize_f(7)
+        first_product(5)
+        empty_agg(5)
         quantize_agg(4, 2)
+        second_product(3)
         add_bias(3)
-        for i in (6, 7):
-            first_product(i)
-            tanh_and_store(i - 4)
-            empty_agg(i, on_vector=i == 6)
-            second_product(i - 2)
-            add_bias(i - 2)
-            quantize_agg(i)
-        for i in (6, 7):
-            tanh_and_store(i - 2)
-            second_product(i)
-            add_bias(i)
-        for i in (6, 7):
-            tanh_and_store(i)
+        turn_back(0)
+        empty_back_and_store(0)
+        turn_back(1)
+        empty_back_and_store(1)
+        tanh_and_store(2)
+        tanh_and_store(3)
+        first_product(6)
+        empty_agg(6, True)
+        second_product(4)
+        add_bias(4)
+        quantize_agg(6)
+        first_product(7)
+        empty_agg(7)
+        tanh_and_store(4)
+        second_product(5)
+        add_bias(5)
+        quantize_agg(7)
+        tanh_and_store(5)
+        second_product(6)
+        add_bias(6)
+        tanh_and_store(6)
+        second_product(7)
+        add_bias(7)
+        tanh_and_store(7)

@@ -94,7 +94,7 @@ def tile_controencodnet_pa_w8_kernel(tc, f_bytes, f_scale, x, w_words, w_scales,
             asc[pair] = keep.tile([P, 2 * P], U8, name="asc%d" % pair, align_bytes=64)
 
         stage = keep.tile([P, 15360], BF16, name="stage", align_bytes=64)
-        f_at = [0, 1024, 2048, 3072, 4096, 5120, 6144, 7168]
+        f_at = [0, 1024, 2048, 3072, 4096, 5120, 11776, 12800]
         a_at = [8192, 8704, 7168, 7680, 9216, 9728, 10240, 10752]
         xg = [stage[:, at : at + T * DIN] for at in (11264, 13312)]
         fc = keep.tile([P, TILES * G * P], U32, name="fc", align_bytes=64)
@@ -133,7 +133,7 @@ def tile_controencodnet_pa_w8_kernel(tc, f_bytes, f_scale, x, w_words, w_scales,
             give(key)
 
         def words_out(i, g0=0, g1=G):
-            plain[i] = ring.tile([P, g1 - g0, P, 2], F32, name="plain", align_bytes=64, bufs=2)
+            plain[i] = ring.tile([P, g1 - g0, P, 2], F32, name="plain", align_bytes=64, bufs=3)
             if ("f", i, g0) in held:
                 nc.scalar.copy(out=plain[i][:], in_=held["f", i, g0][1][:].rearrange("p u g n -> p g n u"))
                 give(("f", i, g0))
@@ -154,8 +154,8 @@ def tile_controencodnet_pa_w8_kernel(tc, f_bytes, f_scale, x, w_words, w_scales,
             nc.vector.quantize_mx(out=fc[:, a:b].bitcast(FP8X4), scales=fsc[:, a:b], in_=stage[:, f_at[i] : f_at[i] + n * NODES])
 
         def interleave_x_gpsimd(g, m0, m1):
-            dst = xg[g].rearrange("p (t m j) -> p t m j", t=T, j=T)[:, :, m0:m1]
-            src = xr[g][:].rearrange("p j (m t) -> p t m j", t=T)[:, :, m0:m1]
+            dst = xg[g].rearrange("p (t m j) -> p m t j", t=T, j=T)[:, m0:m1]
+            src = xr[g][:].rearrange("p j (m t) -> p m t j", t=T)[:, m0:m1]
             nc.gpsimd.tensor_scalar(out=dst, in0=src, scalar1=1.0, scalar2=0.0, op0=MULT, op1=ADD)
 
         def interleave_x(g, m0, m1, on_vector=False):
@@ -174,12 +174,6 @@ def tile_controencodnet_pa_w8_kernel(tc, f_bytes, f_scale, x, w_words, w_scales,
         def empty_x(g, h):
             nc.scalar.copy(out=xg[g].rearrange("p (t n) -> p t n", t=T)[:, :, 2 * P * h : 2 * P * (h + 1)], in_=held["x", g, h][1][:])
             give(("x", g, h))
-
-        def warm_up(n):
-            bank = take("warm", [P, DIN], F32)
-            for r in range(n):
-                nc.tensor.matmul(out=bank[:], lhsT=ident_bf[:], rhs=xr[0][:, r, :], start=True, stop=True)
-            give("warm")
 
         def turn_bias():
             bank = take("bias", [P, P], BF16)
@@ -254,7 +248,7 @@ def tile_controencodnet_pa_w8_kernel(tc, f_bytes, f_scale, x, w_words, w_scales,
             store(i, 0, H)
 
         def column_parts(i):
-            return [(0, H)] if i == TILES - 1 else [(0, H)]
+            return [(0, H // 2), (H // 2, H)] if i == TILES - 1 else [(0, H)]
 
         def add_bias(i):
             summed[i] = ring.tile([P, H], F32, name="summed")
@@ -279,6 +273,7 @@ def tile_controencodnet_pa_w8_kernel(tc, f_bytes, f_scale, x, w_words, w_scales,
         widen(4, engine="scalar")
         widen(5, engine="scalar")
         interleave_x(1, 0, 64)
+        widen(7, 1, 2, "scalar")
         turn(0, 0, 1)
         multiply(0, 0, 1)
         turn(0, 1, 2)
@@ -300,9 +295,12 @@ def tile_controencodnet_pa_w8_kernel(tc, f_bytes, f_scale, x, w_words, w_scales,
         turn(5)
         multiply(5)
         turn_bias()
+        turn(7, 1, 2)
+        words_out(7, 1, 2)
         empty_bias()
         widen(6, engine="scalar")
-        widen(7, engine="scalar")
+        widen(7, 0, 1, "scalar")
+        multiply_on_gpsimd(7, 1, 2)
         first_product(0, 0, 1)
         first_product(1, 0, 1)
         first_product(2, 0, 1)
@@ -317,13 +315,11 @@ def tile_controencodnet_pa_w8_kernel(tc, f_bytes, f_scale, x, w_words, w_scales,
         first_product(3)
         empty_agg(3)
         quantize_agg(2, 2)
-        turn(7, 1, 2)
-        words_out(7, 1, 2)
-        multiply_on_gpsimd(7, 1, 2)
         turn(6)
         multiply(6)
         turn(7, 0, 1)
         multiply(7, 0, 1)
+        quantize_f(6)
         second_product_turned(0, 0)
         tanh_turned(0, 0)
         second_product_turned(0, 1)
@@ -332,7 +328,6 @@ def tile_controencodnet_pa_w8_kernel(tc, f_bytes, f_scale, x, w_words, w_scales,
         empty_agg(4)
         second_product(2)
         add_bias(2)
-        quantize_f(6)
         quantize_f(7)
         first_product(5)
         empty_agg(5)

from contextlib import ExitStack

import concourse.mybir as mybir
from concourse.masks import make_identity

F32 = mybir.dt.float32
BF16 = mybir.dt.bfloat16
U32 = mybir.dt.uint32
I32 = mybir.dt.int32
U8 = mybir.dt.uint8
FP8 = mybir.dt.float8_e4m3fn
FP8X4 = mybir.dt.float8_e4m3fn_x4
MULT = mybir.AluOpType.mult
ADD = mybir.AluOpType.add
ACT = mybir.ActivationFunctionType

P = 128
NODES = 1024
DIN = 512
H = 512
G = 2
T = 4
TILES = 8
BANKS = 8
FLOPS = 2 * NODES * NODES * DIN + 2 * NODES * DIN * H


def tile_controencodnet_pa_w8_kernel(tc, f_bytes, f_scale, x, w_words, w_scales, b1, out):
    nc = tc.nc
    with ExitStack() as ctx:
        keep = ctx.enter_context(tc.tile_pool(name="keep", bufs=1))
        ring = ctx.enter_context(tc.tile_pool(name="ring", bufs=TILES))
        ps = ctx.enter_context(tc.psum_pool(name="ps", bufs=1))
        ctx.enter_context(tc.manual_schedule())

        bytes_src = f_bytes.rearrange("(p i) k -> p (i k)", i=TILES)
        out_dst = out.rearrange("(p i) h -> p i h", i=TILES)
        x_src = x.rearrange("(g p j) d -> g p j d", g=G, j=T)

        loads = [(0, 1024), (1024, 2048), (2048, 4096), (4096, 6144), (6144, 8192)]
        fb = [keep.tile([P, b - a], U8, name="fb%d" % a, align_bytes=64) for a, b in loads]
        fs = keep.tile([P, G, 2 * T], F32, name="fs")
        xr = [keep.tile([P, T, DIN], BF16, name="xr%d" % g, align_bytes=64) for g in range(G)]
        xc = [keep.tile([P, DIN], U32, name="xc%d" % g, align_bytes=64) for g in range(G)]
        xs = [keep.tile([P, DIN], U8, name="xs%d" % g, align_bytes=64) for g in range(G)]
        wc = keep.tile([P, H * T], U8, name="wc", align_bytes=64)
        ws = keep.tile([P, H], U8, name="ws", align_bytes=64)
        bias = keep.tile([P, H], BF16, name="bias")
        bias_col = keep.tile([P, T], F32, name="bias_col")
        bias_rows = keep.tile([P, P], BF16, name="bias_rows")
        ident = keep.tile([P, P], F32, name="ident")
        ident_bf = keep.tile([P, P], BF16, name="ident_bf")

        free_banks = list(range(BANKS))
        held = {}

        def take(key, shape, dtype):
            b = free_banks.pop(0)
            held[key] = (b, ps.tile(shape, dtype, name="bank%d" % b))
            return held[key][1]

        def give(key):
            free_banks.append(held.pop(key)[0])

        def load_f(q):
            a, b = loads[q]
            nc.sync.dma_start(out=fb[q][:], in_=bytes_src[:, a:b])

        def load_x(g):
            nc.sync.dma_start(out=xr[g][:], in_=x_src[g])

        make_identity(nc, ident[:])
        nc.vector.memset(bias_rows[:], 0.0)
        nc.vector.memset(ws[:].bitcast(I32), 0)

        load_f(0)
        nc.sync.dma_start(out=fs[:, :, 0:T], in_=f_scale.rearrange("o (g p t) -> p (o g) t", g=G, t=T))
        load_f(1)
        load_f(2)
        load_x(0)
        load_f(3)
        load_x(1)
        load_f(4)
        nc.sync.dma_start(out=bias_rows[0:T, :], in_=b1.rearrange("(c p) -> c p", c=T))
        nc.sync.dma_start(out=wc[:], in_=w_words[0].rearrange("p n t -> p (n t)"))
        for q in range(4):
            nc.sync.dma_start(out=ws[32 * q : 32 * q + 4, :].bitcast(I32), in_=w_scales[0, 4 * q : 4 * q + 4, :].bitcast(I32))
        nc.sync.dma_start(out=bias[:], in_=b1.partition_broadcast(P))
        nc.vector.tensor_copy(out=ident_bf[:], in_=ident[:])

        wide, ac, asc, summed, res_t, plain = {}, {}, {}, {}, {}, {}
        for pair in range(TILES // 2):
            ac[pair] = keep.tile([P, 2 * P], U32, name="ac%d" % pair, align_bytes=64)
            asc[pair] = keep.tile([P, 2 * P], U8, name="asc%d" % pair, align_bytes=64)

        stage = keep.tile([P, 15360], BF16, name="stage", align_bytes=64)
        f_at = [0, 1024, 2048, 3072, 4096, 5120, 11776, 12800]
        a_at = [8192, 8704, 7168, 7680, 9216, 9728, 10240, 10752]
        xg = [stage[:, at : at + T * DIN] for at in (11264, 13312)]
        fc = keep.tile([P, TILES * G * P], U32, name="fc", align_bytes=64)
        fsc = keep.tile([P, TILES * G * P], U8, name="fsc", align_bytes=64)

        def scaled(i):
            return stage[:, f_at[i] : f_at[i] + NODES]

        def widen(i, g0=0, g1=G, engine="scalar"):
            first, last = NODES * i + DIN * g0, NODES * i + DIN * g1
            q = [a <= first < b for a, b in loads].index(True)
            tile = ring.tile([P, DIN * (g1 - g0)], BF16, name="wide", align_bytes=64, bufs=TILES + 3)
            for g in range(g0, g1):
                wide[i, g] = tile[:, DIN * (g - g0) : DIN * (g - g0 + 1)]
            copy = {"scalar": nc.scalar.copy, "vector": nc.vector.tensor_copy, "gpsimd": nc.gpsimd.tensor_copy}[engine]
            copy(out=tile[:], in_=fb[q][:, first - loads[q][0] : last - loads[q][0]].bitcast(FP8))

        def turn(i, g0=0, g1=G):
            bank = take(("f", i, g0), [P, 2, g1 - g0, P], F32)
            for g in range(g0, g1):
                words = wide[i, g].bitcast(F32)
                for u in range(2):
                    nc.tensor.transpose(bank[:, u, g - g0, :], words[:, u : 2 * P : 2], ident[:])

        def multiply(i, g0=0, g1=G):
            n = g1 - g0
            key = ("f", i, g0) if ("f", i, g0) in held and held["f", i, g0][1].shape[2] == n else ("f", i, 0)
            bank = held[key][1]
            words = bank[:] if bank.shape[2] == n else bank[:, :, g0:g1, :]
            nc.vector.tensor_tensor(
                out=scaled(i)[:, DIN * g0 : DIN * g1].rearrange("p (g n u e) -> p g n u e", g=n, u=2, e=2),
                in0=words.bitcast(BF16).rearrange("p u g (n e) -> p g n u e", e=2),
                in1=fs[:, g0:g1, 0:T].unsqueeze(2).to_broadcast([P, n, P, T]).rearrange("p g n (u e) -> p g n u e", u=2),
                op=MULT,
            )
            give(key)

        def words_out(i, g0=0, g1=G):
            plain[i] = ring.tile([P, g1 - g0, P, 2], F32, name="plain", align_bytes=64, bufs=3)
            if ("f", i, g0) in held:
                nc.scalar.copy(out=plain[i][:], in_=held["f", i, g0][1][:].rearrange("p u g n -> p g n u"))
                give(("f", i, g0))
            else:
                nc.scalar.copy(out=plain[i][:], in_=held["f", i, 0][1][:, :, g0:g1, :].rearrange("p u g n -> p g n u"))

        def multiply_on_gpsimd(i, g0=0, g1=G):
            n = g1 - g0
            nc.gpsimd.tensor_tensor(
                out=scaled(i)[:, DIN * g0 : DIN * g1].rearrange("p (g n t) -> p g n t", g=n, t=T),
                in0=plain[i][:].rearrange("p g n u -> p (g n u)").bitcast(BF16).rearrange("p (g n t) -> p g n t", g=n, t=T),
                in1=fs[:, g0:g1, 0:T].unsqueeze(2).to_broadcast([P, n, P, T]),
                op=MULT,
            )

        def quantize_f(i, n=1):
            a, b = G * P * i, G * P * (i + n)
            nc.vector.quantize_mx(out=fc[:, a:b].bitcast(FP8X4), scales=fsc[:, a:b], in_=stage[:, f_at[i] : f_at[i] + n * NODES])

        def interleave_x_gpsimd(g, m0, m1):
            dst = xg[g].rearrange("p (t m j) -> p m t j", t=T, j=T)[:, m0:m1]
            src = xr[g][:].rearrange("p j (m t) -> p m t j", t=T)[:, m0:m1]
            nc.gpsimd.tensor_scalar(out=dst, in0=src, scalar1=1.0, scalar2=0.0, op0=MULT, op1=ADD)

        def interleave_x(g, m0, m1, on_vector=False):
            dst = xg[g].rearrange("p (t m e j) -> p m t e j", t=T, e=2, j=T)[:, m0 // 2 : m1 // 2]
            src = xr[g][:].rearrange("p j (m e t) -> p m t e j", e=2, t=T)[:, m0 // 2 : m1 // 2]
            copy = nc.vector.tensor_copy if on_vector else nc.scalar.copy
            copy(out=dst, in_=src)

        def interleave_x_tensor(g, h):
            bank = take(("x", g, h), [P, T, 64 * T], BF16)
            src = xr[g][:].rearrange("p j (m t) -> p j m t", t=T)[:, :, 64 * h : 64 * (h + 1)]
            dst = bank[:].rearrange("p t (m j) -> p j m t", j=T)
            for u in range(2):
                nc.tensor.matmul(out=dst[:, 2 * u : 2 * u + 2], lhsT=ident_bf[:], rhs=src[:, 2 * u : 2 * u + 2], start=True, stop=True)

        def empty_x(g, h):
            nc.scalar.copy(out=xg[g].rearrange("p (t n) -> p t n", t=T)[:, :, 2 * P * h : 2 * P * (h + 1)], in_=held["x", g, h][1][:])
            give(("x", g, h))

        def turn_bias():
            bank = take("bias", [P, P], BF16)
            nc.tensor.transpose(bank[:], bias_rows[:], ident_bf[:])

        def empty_bias():
            nc.scalar.copy(out=bias_col[:], in_=held["bias"][1][:, 0:T])
            give("bias")

        def quantize_x(g):
            nc.vector.quantize_mx(out=xc[g][:].bitcast(FP8X4), scales=xs[g][:], in_=xg[g])

        def first_product(i, g0=0, g1=G):
            bank = take(("agg", i), [P, T, P], F32) if g0 == 0 else held["agg", i][1]
            for g in range(g0, g1):
                rows = slice(P * (G * i + g), P * (G * i + g + 1))
                for t in range(T):
                    cols = slice(P * t, P * (t + 1))
                    nc.tensor.matmul_mx(out=bank[:, t, :], lhsT=xc[g][:, cols].bitcast(FP8X4), lhsT_scale=xs[g][:, cols],
                                        rhs=fc[:, rows].bitcast(FP8X4), rhs_scale=fsc[:, rows], start=(g == 0 and t == 0), stop=(g == G - 1 and t == T - 1))

        def empty_agg(i, on_vector=False):
            dst = stage[:, a_at[i] : a_at[i] + DIN]
            copy = nc.vector.tensor_copy if on_vector else nc.scalar.copy
            copy(out=dst.rearrange("p (n t) -> p n t", t=T), in_=held["agg", i][1][:].rearrange("p t n -> p n t"))
            give(("agg", i))

        def quantize_agg(i, n=1):
            a, b = P * (i % 2), P * (i % 2 + n)
            nc.vector.quantize_mx(out=ac[i // 2][:, a:b].bitcast(FP8X4), scales=asc[i // 2][:, a:b], in_=stage[:, a_at[i] : a_at[i] + n * DIN])

        def second_product(i):
            bank = take(("prod", i), [P, H], F32)
            rows = slice(P * (i % 2), P * (i % 2 + 1))
            nc.tensor.matmul_mx(out=bank[:], lhsT=ac[i // 2][:, rows].bitcast(FP8X4), lhsT_scale=asc[i // 2][:, rows], rhs=wc[:].bitcast(FP8X4), rhs_scale=ws[:], start=True, stop=True)

        def second_product_turned(pair, half):
            bank = take(("prod_t", pair, half), [P, 2, 2 * P], F32)
            for c in range(2 * half, 2 * half + 2):
                nc.tensor.matmul_mx(out=bank[:, c % 2, :], lhsT=wc[:, T * P * c : T * P * (c + 1)].bitcast(FP8X4), lhsT_scale=ws[:, P * c : P * (c + 1)],
                                    rhs=ac[pair][:].bitcast(FP8X4), rhs_scale=asc[pair][:], start=True, stop=True)

        def tanh_turned(pair, half):
            for c in range(2 * half, 2 * half + 2):
                res_t[pair, c] = ring.tile([P, 2 * P], F32, name="res_t")
                nc.scalar.activation(out=res_t[pair, c][:], in_=held["prod_t", pair, half][1][:, c % 2, :], func=ACT.Tanh, bias=bias_col[:, c : c + 1])
            give(("prod_t", pair, half))

        def turn_back(i):
            bank = take(("back", i), [P, H], F32)
            for c in reversed(range(T)):
                nc.tensor.transpose(bank[:, P * c : P * (c + 1)], res_t[i // 2, c][:, P * (i % 2) : P * (i % 2 + 1)], ident[:])

        results = {}

        def result(i):
            if i // 2 not in results:
                results[i // 2] = keep.tile([P, 2, H], F32, name="res%d" % (i // 2))
            return results[i // 2][:, i % 2, :]

        def store(i, a, b):
            if i // 2 not in ():
                nc.sync.dma_start(out=out_dst[:, i, a:b], in_=result(i)[:, a:b])
            elif i % 2 == 1:
                nc.sync.dma_start(out=out_dst[:, i - 1 : i + 1, :], in_=results[i // 2][:])

        def empty_back_and_store(i, on_vector=False):
            res = result(i)
            copy = nc.vector.tensor_copy if on_vector else nc.scalar.copy
            copy(out=res, in_=held["back", i][1][:])
            give(("back", i))
            store(i, 0, H)

        def column_parts(i):
            return [(0, H // 2), (H // 2, H)] if i == TILES - 1 else [(0, H)]

        def add_bias(i):
            summed[i] = ring.tile([P, H], F32, name="summed")
            for a, b in column_parts(i):
                nc.vector.tensor_tensor(out=summed[i][:, a:b], in0=held["prod", i][1][:, a:b], in1=bias[:, a:b], op=ADD)
            give(("prod", i))

        def tanh_and_store(i):
            res = result(i)
            for a, b in column_parts(i):
                nc.scalar.activation(out=res[:, a:b], in_=summed[i][:, a:b], func=ACT.Tanh)
                store(i, a, b)

        interleave_x_gpsimd(0, 0, 88)
        widen(0, 1, 2, "vector")
        widen(1, 0, 1, "vector")
        widen(0, 0, 1, "scalar")
        widen(1, 1, 2, "scalar")
        widen(2, engine="scalar")
        widen(3, engine="scalar")
        interleave_x(0, 88, 128)
        widen(4, engine="scalar")
        widen(5, engine="scalar")
        interleave_x(1, 0, 64)
        widen(7, 1, 2, "scalar")
        turn(0, 0, 1)
        multiply(0, 0, 1)
        turn(0, 1, 2)
        multiply(0, 1, 2)
        turn(1)
        multiply(1)
        turn(2)
        multiply(2)
        turn(3)
        multiply(3)
        quantize_f(0, 2)
        quantize_x(0)
        quantize_f(2, 2)
        interleave_x_tensor(1, 1)
        empty_x(1, 1)
        quantize_x(1)
        turn(4)
        multiply(4)
        turn(5)
        multiply(5)
        turn_bias()
        turn(7, 1, 2)
        words_out(7, 1, 2)
        empty_bias()
        widen(6, engine="scalar")
        widen(7, 0, 1, "scalar")
        multiply_on_gpsimd(7, 1, 2)
        first_product(0, 0, 1)
        first_product(1, 0, 1)
        first_product(2, 0, 1)
        first_product(0, 1, 2)
        empty_agg(0)
        first_product(1, 1, 2)
        empty_agg(1)
        quantize_agg(0, 2)
        quantize_f(4, 2)
        first_product(2, 1, 2)
        empty_agg(2)
        first_product(3)
        empty_agg(3)
        quantize_agg(2, 2)
        turn(6)
        multiply(6)
        turn(7, 0, 1)
        multiply(7, 0, 1)
        quantize_f(6)
        second_product_turned(0, 0)
        tanh_turned(0, 0)
        second_product_turned(0, 1)
        tanh_turned(0, 1)
        first_product(4)
        empty_agg(4)
        second_product(2)
        add_bias(2)
        quantize_f(7)
        first_product(5)
        empty_agg(5)
        quantize_agg(4, 2)
        second_product(3)
        add_bias(3)
        turn_back(0)
        empty_back_and_store(0)
        turn_back(1)
        empty_back_and_store(1)
        tanh_and_store(2)
        tanh_and_store(3)
        first_product(6)
        empty_agg(6, True)
        second_product(4)
        add_bias(4)
        quantize_agg(6)
        first_product(7)
        empty_agg(7)
        tanh_and_store(4)
        second_product(5)
        add_bias(5)
        quantize_agg(7)
        tanh_and_store(5)
        second_product(6)
        add_bias(6)
        tanh_and_store(6)
        second_product(7)
        add_bias(7)
        tanh_and_store(7)
